import numpy as np
import ml_dtypes


def mxq(x, axis, fmt="e4m3"):
    dtype, down = {"e4m3": (ml_dtypes.float8_e4m3fn, 7), "e5m2": (ml_dtypes.float8_e5m2, 14)}[fmt]
    v = np.moveaxis(np.asarray(x, np.float32).astype(ml_dtypes.bfloat16).astype(np.float64), axis, -1)
    blocks = v.reshape(v.shape[:-1] + (-1, 32))
    amax = np.abs(blocks).max(-1, keepdims=True)
    byte = np.maximum(np.where(amax > 0, np.frexp(amax)[1] - 1 + 127, 0) - down, 1)
    scale = np.exp2(byte - 127.0)
    codes = (blocks / scale).astype(np.float32).astype(dtype).astype(np.float64)
    return np.moveaxis((codes * scale).reshape(v.shape), -1, axis)


WIDE = False


def mx_kscale(k):
    if not WIDE:
        return np.ones(k)
    levels = np.array([10, -10, 5, -5, 0])
    a = np.random.permutation(np.resize(levels, k // 512 * 4)).reshape(k // 512, 4)
    idx = np.arange(k)
    return np.exp2(a[idx // 512, idx % 128 // 32])


BF16 = ml_dtypes.bfloat16


def bf(x):
    return np.asarray(x, np.float32).astype(BF16)


def f64(x):
    return np.asarray(x).astype(np.float64)


B, N, C, H, R, BLK = 32, 256, 512, 16, 128, 16


def setup_inputs():
    s, t = mx_kscale(C), mx_kscale(C)
    return {"wv": bf(np.random.standard_normal((B, N, C)) * 0.12),
            "x": bf(np.random.standard_normal((B, N, C)) * t),
            "dw_w": bf(np.random.standard_normal(C) * 6.0 * s),
            "dw_b": bf(np.random.standard_normal(C) * 0.4 * s),
            "pw_w": bf(np.random.standard_normal((C, C)) / np.sqrt(C) * t[:, None] / s[None, :]),
            "pw_b": bf(np.random.standard_normal(C) * 0.3 * t),
            "p_w1": bf(np.random.standard_normal((R, C)) / np.sqrt(C) / t[None, :])}


def reference(wv, x, dw_w, dw_b, pw_w, pw_b, p_w1):
    a = f64(wv) * f64(dw_w) + f64(dw_b)
    dyn = (mxq(a, 2, "e4m3") @ mxq(f64(pw_w), 1, "e4m3").T) + f64(pw_b)
    y = dyn + f64(x)
    return mxq(y, 2, "e4m3") @ mxq(f64(p_w1), 1, "e4m3").T

@@ -1,0 +1,287 @@
+from contextlib import ExitStack
+
+import concourse.masks as masks
+import concourse.mybir as mybir
+
+F32 = mybir.dt.float32
+BF16 = mybir.dt.bfloat16
+U32 = mybir.dt.uint32
+U8 = mybir.dt.uint8
+FP8X4 = mybir.dt.float8_e4m3fn_x4
+IDENTITY = mybir.ActivationFunctionType.Identity
+ADD = mybir.AluOpType.add
+
+P = 128
+PACK = 4
+CHANNELS = P * PACK
+RANK = 128
+TOKENS = 32 * 256
+CHUNK = 512
+TILES = CHUNK // P
+HALF = CHUNK // 2
+N_CHUNKS = TOKENS // CHUNK
+
+FLOPS = 2 * TOKENS * CHANNELS * CHANNELS + 2 * TOKENS * CHANNELS * RANK
+
+
+def tile_dssattention_pa_t_kernel(tc, wv, x, dw_w, dw_b, pw_w, pw_b, p_w1, out):
+    nc = tc.nc
+
+    wv_chunks = wv.flatten_outer_dims().rearrange("(c p q) k -> c p (q k)", p=P, q=TILES)
+    x_chunks = x.flatten_outer_dims().rearrange("(c p q) k -> c p (q k)", p=P, q=TILES)
+    out_chunks = out.flatten_outer_dims().rearrange("(c p q) r -> c p (q r)", p=P, q=TILES)
+
+    with ExitStack() as stack:
+        const = stack.enter_context(tc.tile_pool(name="const", bufs=1))
+        loads = stack.enter_context(tc.tile_pool(name="loads", bufs=4))
+        work = stack.enter_context(tc.tile_pool(name="work", bufs=3))
+        psum_wv = stack.enter_context(tc.psum_pool(name="psum_wv", bufs=2))
+        psum_x = stack.enter_context(tc.psum_pool(name="psum_x", bufs=2))
+        psum_dyn = stack.enter_context(tc.psum_pool(name="psum_dyn", bufs=3))
+        psum_out = stack.enter_context(tc.psum_pool(name="psum_out", bufs=1))
+
+        wv_rows, x_rows, wv_t, x_t = {}, {}, {}, {}
+        a_planes, a_codes, a_scales = {}, {}, {}
+        dyn, dyn_biased, y_grouped, y_codes, y_scales, out_acc = {}, {}, {}, {}, {}, {}
+        a_grouped = {}
+
+        def live(c):
+            return 0 <= c < N_CHUNKS
+
+
+        def transpose_channel_planes(rows, h):
+            bank = psum_wv.tile([P, 2, CHUNK], BF16, tag="wv_t")
+            for i in range(2):
+                t = 2 * h + i
+                for q in range(TILES):
+                    nc.tensor.transpose(
+                        bank[:, i, q * P : (q + 1) * P], rows[:, q, t * P : (t + 1) * P], ident_bf16[:]
+                    )
+            return bank
+
+        def group_planes(grouped, planes):
+            nc.vector.tensor_copy(
+                out=grouped[:].rearrange("p (c i) t -> p c t i", i=4),
+                in_=planes[:].rearrange("p t (c i) -> p c t i", i=4),
+            )
+
+        def quantise(codes, scales, grouped):
+            nc.vector.quantize_mx(
+                out=codes[:].bitcast(FP8X4),
+                scales=scales[:],
+                in_=grouped[:].rearrange("p w t -> p (w t)"),
+            )
+
+
+        def load_wv(c):
+            if not live(c):
+                return
+            rows = loads.tile([P, TILES, CHANNELS], BF16, tag="wv_rows")
+            nc.sync.dma_start(out=rows[:].rearrange("p q k -> p (q k)"), in_=wv_chunks[c])
+            wv_rows[c] = rows
+
+        def load_x(c):
+            if not live(c):
+                return
+            rows = loads.tile([P, TILES, CHANNELS], BF16, tag="x_rows")
+            nc.sync.dma_start(out=rows[:].rearrange("p q k -> p (q k)"), in_=x_chunks[c])
+            x_rows[c] = rows
+
+
+        ident_bf16 = const.tile([P, P], BF16)
+        masks.make_identity(nc, ident_bf16[:])
+        ident_f32 = const.tile([P, P], F32)
+        masks.make_identity(nc, ident_f32[:])
+
+        vectors = const.tile([P, CHANNELS], BF16)
+        nc.vector.memset(vectors[:], 0.0)
+        for row, vector in enumerate((dw_w, dw_b, pw_b)):
+            nc.sync.dma_start(out=vectors[row : row + 1, :], in_=vector.rearrange("(o k) -> o k", o=1))
+
+        pw_rows = const.tile([P, PACK, CHANNELS], BF16)
+        nc.sync.dma_start(
+            out=pw_rows[:].rearrange("m (u e) k -> m u (e k)", u=2),
+            in_=pw_w.rearrange("(u m e) k -> m u (e k)", u=2, e=2),
+        )
+        load_wv(0)
+        p1_rows = const.tile([P, CHANNELS], BF16)
+        nc.sync.dma_start(out=p1_rows[:], in_=p_w1)
+        load_wv(1)
+
+        vectors_t = psum_wv.tile([P, 2, CHUNK], BF16, tag="wv_t")
+        for t in range(PACK):
+            nc.tensor.transpose(
+                vectors_t[:, 0, t * P : (t + 1) * P], vectors[:, t * P : (t + 1) * P], ident_bf16[:]
+            )
+        dw = const.tile([P, PACK, 2], F32)
+        nc.vector.tensor_copy(
+            out=dw[:], in_=vectors_t[:, 0, :].rearrange("p (t r) -> p t r", t=PACK)[:, :, 0:2]
+        )
+
+        words_t = psum_x.tile([P, 2, HALF], F32, tag="x_t")
+        for u in range(2):
+            word_cols = slice(u * P, (u + 1) * P)
+            nc.tensor.transpose(words_t[:, u, 0:P], vectors[:].bitcast(F32)[:, word_cols], ident_f32[:])
+            nc.tensor.transpose(words_t[:, u, P : 2 * P], p1_rows[:].bitcast(F32)[:, word_cols], ident_f32[:])
+        pw_bias = const.tile([P, 2, 2], F32)
+        nc.vector.tensor_copy(out=pw_bias[:], in_=words_t[:].bitcast(BF16)[:, :, 4:6])
+        p1_grouped = const.tile([P, RANK, PACK], BF16, align_bytes=64)
+        nc.vector.tensor_copy(
+            out=p1_grouped[:].bitcast(F32), in_=words_t[:, :, P : 2 * P].rearrange("p u r -> p r u")
+        )
+
+        pw_planes = const.tile([P, PACK, CHUNK], BF16)
+        for h in range(2):
+            bank = transpose_channel_planes(pw_rows, h)
+            nc.vector.tensor_copy(out=pw_planes[:, 2 * h : 2 * h + 2, :], in_=bank[:])
+        pw_grouped = const.tile([P, CHUNK, PACK], BF16, align_bytes=64)
+        group_planes(pw_grouped, pw_planes)
+
+        p1_codes = const.tile([P, RANK], U32, align_bytes=64)
+        p1_scales = const.tile([P, RANK], U8, align_bytes=64)
+        quantise(p1_codes, p1_scales, p1_grouped)
+        pw_codes = const.tile([P, CHUNK], U32, align_bytes=64)
+        pw_scales = const.tile([P, CHUNK], U8, align_bytes=64)
+        quantise(pw_codes, pw_scales, pw_grouped)
+
+
+        def transpose_wv(c, h):
+            if live(c):
+                wv_t[c, h] = transpose_channel_planes(wv_rows[c], h)
+
+        def affine(c, h):
+            if not live(c):
+                return
+            if h == 0:
+                planes = work.tile([P, PACK, CHUNK], BF16, tag="a_planes")
+                a_planes[c] = planes
+            for i in range(2):
+                t = 2 * h + i
+                nc.scalar.activation(
+                    out=a_planes[c][:, t, :],
+                    in_=wv_t[c, h][:, i, :],
+                    func=IDENTITY,
+                    scale=dw[:, t, 0:1],
+                    bias=dw[:, t, 1:2],
+                )
+
+        def group_a(c):
+            if not live(c):
+                return
+            grouped = work.tile([P, CHUNK, PACK], BF16, tag="a_grouped", align_bytes=64)
+            group_planes(grouped, a_planes[c])
+            a_grouped[c] = grouped
+
+        def quantise_a(c):
+            if not live(c):
+                return
+            codes = work.tile([P, CHUNK], U32, tag="a_codes", align_bytes=64)
+            scales = work.tile([P, CHUNK], U8, tag="a_scales", align_bytes=64)
+            quantise(codes, scales, a_grouped[c])
+            a_codes[c], a_scales[c] = codes, scales
+
+        def first_matmul(c, j):
+            if not live(c):
+                return
+            acc = psum_dyn.tile([P, CHUNK], F32, tag="dyn")
+            nc.tensor.matmul_mx(
+                out=acc[:],
+                lhsT=pw_codes[:, j * P : (j + 1) * P].bitcast(FP8X4),
+                lhsT_scale=pw_scales[:, j * P : (j + 1) * P],
+                rhs=a_codes[c][:].bitcast(FP8X4),
+                rhs_scale=a_scales[c][:],
+                start=True,
+                stop=True,
+            )
+            dyn[c, j] = acc
+
+        def add_bias(c, j):
+            if not live(c):
+                return
+            if j == 0:
+                biased = work.tile([P, PACK, CHUNK], F32, tag="dyn_biased")
+                dyn_biased[c] = biased
+            nc.scalar.activation(
+                out=dyn_biased[c][:, j, :],
+                in_=dyn[c, j][:],
+                func=IDENTITY,
+                scale=1.0,
+                bias=pw_bias[:, j // 2, j % 2 : j % 2 + 1],
+            )
+
+        def transpose_x(c, h):
+            if not live(c):
+                return
+            bank = psum_x.tile([P, 2, HALF], F32, tag="x_t")
+            words = x_rows[c][:].bitcast(F32)
+            for u in range(2):
+                for i in range(2):
+                    nc.tensor.transpose(
+                        bank[:, u, i * P : (i + 1) * P], words[:, 2 * h + i, u * P : (u + 1) * P], ident_f32[:]
+                    )
+            x_t[c, h] = bank
+
+        def add_x(c, h):
+            if not live(c):
+                return
+            if h == 0:
+                grouped = work.tile([P, CHUNK, PACK], BF16, tag="y_grouped", align_bytes=64)
+                y_grouped[c] = grouped
+            tokens = slice(h * HALF, (h + 1) * HALF)
+            nc.vector.tensor_tensor(
+                out=y_grouped[c][:, tokens, :].rearrange("p w (u e) -> p w u e", u=2),
+                in0=x_t[c, h][:].bitcast(BF16).rearrange("p u (w e) -> p w u e", e=2),
+                in1=dyn_biased[c][:, :, tokens].rearrange("p (u e) w -> p w u e", u=2),
+                op=ADD,
+            )
+
+        def quantise_y(c):
+            if not live(c):
+                return
+            codes = work.tile([P, CHUNK], U32, tag="y_codes", align_bytes=64)
+            scales = work.tile([P, CHUNK], U8, tag="y_scales", align_bytes=64)
+            quantise(codes, scales, y_grouped[c])
+            y_codes[c], y_scales[c] = codes, scales
+
+        def second_matmul(c):
+            if not live(c):
+                return
+            acc = psum_out.tile([P, TILES, RANK], F32, tag="out_acc")
+            for q in range(TILES):
+                nc.tensor.matmul_mx(
+                    out=acc[:, q, :],
+                    lhsT=y_codes[c][:, q * P : (q + 1) * P].bitcast(FP8X4),
+                    lhsT_scale=y_scales[c][:, q * P : (q + 1) * P],
+                    rhs=p1_codes[:].bitcast(FP8X4),
+                    rhs_scale=p1_scales[:],
+                    start=True,
+                    stop=True,
+                )
+            out_acc[c] = acc
+
+        def store(c):
+            if not live(c):
+                return
+            result = work.tile([P, TILES, RANK], F32, tag="result")
+            nc.scalar.copy(out=result[:], in_=out_acc[c][:])
+            nc.gpsimd.dma_start(out=out_chunks[c], in_=result[:].rearrange("p q r -> p (q r)"))
+
+        for n in range(-1, N_CHUNKS + 4):
+            load_wv(n + 3)
+            load_x(n)
+            for j in range(3):
+                first_matmul(n - 2, j)
+            second_matmul(n - 4)
+            for h in range(2):
+                affine(n, h)
+                add_x(n - 3, h)
+                transpose_wv(n + 1, h)
+                transpose_x(n - 2, h)
+            group_a(n - 1)
+            add_bias(n - 2, 0)
+            first_matmul(n - 2, 3)
+            for j in range(1, PACK):
+                add_bias(n - 2, j)
+            quantise_y(n - 3)
+            quantise_a(n - 1)
+            store(n - 4)

@@ -37,8 +37,9 @@ def tile_dssattention_pa_t_kernel(tc, wv, x, dw_w, dw_b, pw_w, pw_b, p_w1, out):
         work = stack.enter_context(tc.tile_pool(name="work", bufs=3))
         psum_wv = stack.enter_context(tc.psum_pool(name="psum_wv", bufs=2))
         psum_x = stack.enter_context(tc.psum_pool(name="psum_x", bufs=2))
-        psum_dyn = stack.enter_context(tc.psum_pool(name="psum_dyn", bufs=3))
-        psum_out = stack.enter_context(tc.psum_pool(name="psum_out", bufs=1))
+        psum_dyn = stack.enter_context(tc.psum_pool(name="psum_dyn", bufs=2))
+        psum_out = stack.enter_context(tc.psum_pool(name="psum_out", bufs=2))
+        stack.enter_context(tc.manual_schedule())
 
         wv_rows, x_rows, wv_t, x_t = {}, {}, {}, {}
         a_planes, a_codes, a_scales = {}, {}, {}
@@ -49,15 +50,13 @@ def tile_dssattention_pa_t_kernel(tc, wv, x, dw_w, dw_b, pw_w, pw_b, p_w1, out):
             return 0 <= c < N_CHUNKS
 
 
-        def transpose_channel_planes(rows, h):
-            bank = psum_wv.tile([P, 2, CHUNK], BF16, tag="wv_t")
+        def transpose_channel_planes(bank, rows, h):
             for i in range(2):
                 t = 2 * h + i
                 for q in range(TILES):
                     nc.tensor.transpose(
                         bank[:, i, q * P : (q + 1) * P], rows[:, q, t * P : (t + 1) * P], ident_bf16[:]
                     )
-            return bank
 
         def group_planes(grouped, planes):
             nc.vector.tensor_copy(
@@ -98,17 +97,17 @@ def tile_dssattention_pa_t_kernel(tc, wv, x, dw_w, dw_b, pw_w, pw_b, p_w1, out):
         for row, vector in enumerate((dw_w, dw_b, pw_b)):
             nc.sync.dma_start(out=vectors[row : row + 1, :], in_=vector.rearrange("(o k) -> o k", o=1))
 
+        load_wv(0)
         pw_rows = const.tile([P, PACK, CHANNELS], BF16)
         nc.sync.dma_start(
             out=pw_rows[:].rearrange("m (u e) k -> m u (e k)", u=2),
             in_=pw_w.rearrange("(u m e) k -> m u (e k)", u=2, e=2),
         )
-        load_wv(0)
+        load_wv(1)
         p1_rows = const.tile([P, CHANNELS], BF16)
         nc.sync.dma_start(out=p1_rows[:], in_=p_w1)
-        load_wv(1)
 
-        vectors_t = psum_wv.tile([P, 2, CHUNK], BF16, tag="wv_t")
+        vectors_t = psum_dyn.tile([P, 2, CHUNK], BF16, tag="dyn")
         for t in range(PACK):
             nc.tensor.transpose(
                 vectors_t[:, 0, t * P : (t + 1) * P], vectors[:, t * P : (t + 1) * P], ident_bf16[:]
@@ -118,36 +117,43 @@ def tile_dssattention_pa_t_kernel(tc, wv, x, dw_w, dw_b, pw_w, pw_b, p_w1, out):
             out=dw[:], in_=vectors_t[:, 0, :].rearrange("p (t r) -> p t r", t=PACK)[:, :, 0:2]
         )
 
-        words_t = psum_x.tile([P, 2, HALF], F32, tag="x_t")
-        for u in range(2):
-            word_cols = slice(u * P, (u + 1) * P)
-            nc.tensor.transpose(words_t[:, u, 0:P], vectors[:].bitcast(F32)[:, word_cols], ident_f32[:])
-            nc.tensor.transpose(words_t[:, u, P : 2 * P], p1_rows[:].bitcast(F32)[:, word_cols], ident_f32[:])
         pw_bias = const.tile([P, 2, 2], F32)
-        nc.vector.tensor_copy(out=pw_bias[:], in_=words_t[:].bitcast(BF16)[:, :, 4:6])
-        p1_grouped = const.tile([P, RANK, PACK], BF16, align_bytes=64)
-        nc.vector.tensor_copy(
-            out=p1_grouped[:].bitcast(F32), in_=words_t[:, :, P : 2 * P].rearrange("p u r -> p r u")
-        )
-
-        pw_planes = const.tile([P, PACK, CHUNK], BF16)
-        for h in range(2):
-            bank = transpose_channel_planes(pw_rows, h)
-            nc.vector.tensor_copy(out=pw_planes[:, 2 * h : 2 * h + 2, :], in_=bank[:])
-        pw_grouped = const.tile([P, CHUNK, PACK], BF16, align_bytes=64)
-        group_planes(pw_grouped, pw_planes)
-
         p1_codes = const.tile([P, RANK], U32, align_bytes=64)
         p1_scales = const.tile([P, RANK], U8, align_bytes=64)
-        quantise(p1_codes, p1_scales, p1_grouped)
         pw_codes = const.tile([P, CHUNK], U32, align_bytes=64)
         pw_scales = const.tile([P, CHUNK], U8, align_bytes=64)
-        quantise(pw_codes, pw_scales, pw_grouped)
+
+        def prepare_weights():
+            pw_planes = const.tile([P, PACK, CHUNK], BF16)
+            for h in range(2):
+                bank = psum_dyn.tile([P, 2, CHUNK], BF16, tag="dyn")
+                transpose_channel_planes(bank, pw_rows, h)
+                nc.vector.tensor_copy(out=pw_planes[:, 2 * h : 2 * h + 2, :], in_=bank[:])
+            pw_grouped = const.tile([P, CHUNK, PACK], BF16, align_bytes=64)
+            group_planes(pw_grouped, pw_planes)
+
+            words_t = psum_out.tile([P, 2, HALF], F32, tag="out_acc")
+            for u in range(2):
+                word_cols = slice(u * P, (u + 1) * P)
+                nc.tensor.transpose(words_t[:, u, 0:P], vectors[:].bitcast(F32)[:, word_cols], ident_f32[:])
+                nc.tensor.transpose(
+                    words_t[:, u, P : 2 * P], p1_rows[:].bitcast(F32)[:, word_cols], ident_f32[:]
+                )
+            nc.vector.tensor_copy(out=pw_bias[:], in_=words_t[:].bitcast(BF16)[:, :, 4:6])
+            p1_grouped = const.tile([P, RANK, PACK], BF16, align_bytes=64)
+            nc.vector.tensor_copy(
+                out=p1_grouped[:].bitcast(F32), in_=words_t[:, :, P : 2 * P].rearrange("p u r -> p r u")
+            )
+            quantise(pw_codes, pw_scales, pw_grouped)
+            quantise(p1_codes, p1_scales, p1_grouped)
 
 
         def transpose_wv(c, h):
-            if live(c):
-                wv_t[c, h] = transpose_channel_planes(wv_rows[c], h)
+            if not live(c):
+                return
+            bank = psum_wv.tile([P, 2, CHUNK], BF16, tag="wv_t")
+            transpose_channel_planes(bank, wv_rows[c], h)
+            wv_t[c, h] = bank
 
         def affine(c, h):
             if not live(c):
@@ -266,22 +272,36 @@ def tile_dssattention_pa_t_kernel(tc, wv, x, dw_w, dw_b, pw_w, pw_b, p_w1, out):
             nc.scalar.copy(out=result[:], in_=out_acc[c][:])
             nc.gpsimd.dma_start(out=out_chunks[c], in_=result[:].rearrange("p q r -> p (q r)"))
 
-        for n in range(-1, N_CHUNKS + 4):
+
+        def step(n):
             load_wv(n + 3)
             load_x(n)
-            for j in range(3):
-                first_matmul(n - 2, j)
-            second_matmul(n - 4)
-            for h in range(2):
-                affine(n, h)
-                add_x(n - 3, h)
-                transpose_wv(n + 1, h)
-                transpose_x(n - 2, h)
-            group_a(n - 1)
+
+            first_matmul(n - 2, 0)
+            first_matmul(n - 2, 1)
+            affine(n, 0)
+            add_x(n - 3, 0)
+            transpose_wv(n, 1)
+            transpose_x(n - 2, 0)
             add_bias(n - 2, 0)
+            add_bias(n - 2, 1)
+            group_a(n - 1)
+
+            first_matmul(n - 2, 2)
             first_matmul(n - 2, 3)
-            for j in range(1, PACK):
-                add_bias(n - 2, j)
-            quantise_y(n - 3)
+            second_matmul(n - 4)
+            affine(n, 1)
+            add_x(n - 3, 1)
+            transpose_wv(n + 1, 0)
+            transpose_x(n - 2, 1)
+            add_bias(n - 2, 2)
+            add_bias(n - 2, 3)
             quantise_a(n - 1)
+            quantise_y(n - 3)
             store(n - 4)
+
+        step(-1)
+        step(0)
+        prepare_weights()
+        for n in range(1, N_CHUNKS + 4):
+            step(n)

@@ -10,6 +10,7 @@ U8 = mybir.dt.uint8
 FP8X4 = mybir.dt.float8_e4m3fn_x4
 IDENTITY = mybir.ActivationFunctionType.Identity
 ADD = mybir.AluOpType.add
+MULT = mybir.AluOpType.mult
 
 P = 128
 PACK = 4
@@ -163,13 +164,23 @@ def tile_dssattention_pa_t_kernel(tc, wv, x, dw_w, dw_b, pw_w, pw_b, p_w1, out):
                 a_planes[c] = planes
             for i in range(2):
                 t = 2 * h + i
-                nc.scalar.activation(
-                    out=a_planes[c][:, t, :],
-                    in_=wv_t[c, h][:, i, :],
-                    func=IDENTITY,
-                    scale=dw[:, t, 0:1],
-                    bias=dw[:, t, 1:2],
-                )
+                if h == 0:
+                    nc.scalar.activation(
+                        out=a_planes[c][:, t, :],
+                        in_=wv_t[c, h][:, i, :],
+                        func=IDENTITY,
+                        scale=dw[:, t, 0:1],
+                        bias=dw[:, t, 1:2],
+                    )
+                else:
+                    nc.vector.tensor_scalar(
+                        out=a_planes[c][:, t, :],
+                        in0=wv_t[c, h][:, i, :],
+                        scalar1=dw[:, t, 0:1],
+                        scalar2=dw[:, t, 1:2],
+                        op0=MULT,
+                        op1=ADD,
+                    )
 
         def group_a(c):
             if not live(c):

@@ -10,7 +10,6 @@ U8 = mybir.dt.uint8
 FP8X4 = mybir.dt.float8_e4m3fn_x4
 IDENTITY = mybir.ActivationFunctionType.Identity
 ADD = mybir.AluOpType.add
-MULT = mybir.AluOpType.mult
 
 P = 128
 PACK = 4
@@ -90,8 +89,6 @@ def tile_dssattention_pa_t_kernel(tc, wv, x, dw_w, dw_b, pw_w, pw_b, p_w1, out):
 
         ident_bf16 = const.tile([P, P], BF16)
         masks.make_identity(nc, ident_bf16[:])
-        ident_f32 = const.tile([P, P], F32)
-        masks.make_identity(nc, ident_f32[:])
 
         vectors = const.tile([P, CHANNELS], BF16)
         nc.vector.memset(vectors[:], 0.0)
@@ -100,10 +97,7 @@ def tile_dssattention_pa_t_kernel(tc, wv, x, dw_w, dw_b, pw_w, pw_b, p_w1, out):
 
         load_wv(0)
         pw_rows = const.tile([P, PACK, CHANNELS], BF16)
-        nc.sync.dma_start(
-            out=pw_rows[:].rearrange("m (u e) k -> m u (e k)", u=2),
-            in_=pw_w.rearrange("(u m e) k -> m u (e k)", u=2, e=2),
-        )
+        nc.sync.dma_start(out=pw_rows[:], in_=pw_w.rearrange("(j m) k -> m j k", m=P))
         load_wv(1)
         p1_rows = const.tile([P, CHANNELS], BF16)
         nc.sync.dma_start(out=p1_rows[:], in_=p_w1)
@@ -113,12 +107,11 @@ def tile_dssattention_pa_t_kernel(tc, wv, x, dw_w, dw_b, pw_w, pw_b, p_w1, out):
             nc.tensor.transpose(
                 vectors_t[:, 0, t * P : (t + 1) * P], vectors[:, t * P : (t + 1) * P], ident_bf16[:]
             )
-        dw = const.tile([P, PACK, 2], F32)
+        per_channel = const.tile([P, PACK, 3], F32)
         nc.vector.tensor_copy(
-            out=dw[:], in_=vectors_t[:, 0, :].rearrange("p (t r) -> p t r", t=PACK)[:, :, 0:2]
+            out=per_channel[:], in_=vectors_t[:, 0, :].rearrange("p (t r) -> p t r", t=PACK)[:, :, 0:3]
         )
 
-        pw_bias = const.tile([P, 2, 2], F32)
         p1_codes = const.tile([P, RANK], U32, align_bytes=64)
         p1_scales = const.tile([P, RANK], U8, align_bytes=64)
         pw_codes = const.tile([P, CHUNK], U32, align_bytes=64)
@@ -133,18 +126,14 @@ def tile_dssattention_pa_t_kernel(tc, wv, x, dw_w, dw_b, pw_w, pw_b, p_w1, out):
             pw_grouped = const.tile([P, CHUNK, PACK], BF16, align_bytes=64)
             group_planes(pw_grouped, pw_planes)
 
-            words_t = psum_out.tile([P, 2, HALF], F32, tag="out_acc")
-            for u in range(2):
-                word_cols = slice(u * P, (u + 1) * P)
-                nc.tensor.transpose(words_t[:, u, 0:P], vectors[:].bitcast(F32)[:, word_cols], ident_f32[:])
-                nc.tensor.transpose(
-                    words_t[:, u, P : 2 * P], p1_rows[:].bitcast(F32)[:, word_cols], ident_f32[:]
-                )
-            nc.vector.tensor_copy(out=pw_bias[:], in_=words_t[:].bitcast(BF16)[:, :, 4:6])
+            p1_t = psum_out.tile([P, PACK, RANK], BF16, tag="out_acc")
+            for t in range(PACK):
+                nc.tensor.transpose(p1_t[:, t, :], p1_rows[:, t * P : (t + 1) * P], ident_bf16[:])
+            p1_planes = const.tile([P, PACK, RANK], BF16)
+            nc.vector.tensor_copy(out=p1_planes[:], in_=p1_t[:])
             p1_grouped = const.tile([P, RANK, PACK], BF16, align_bytes=64)
-            nc.vector.tensor_copy(
-                out=p1_grouped[:].bitcast(F32), in_=words_t[:, :, P : 2 * P].rearrange("p u r -> p r u")
-            )
+            group_planes(p1_grouped, p1_planes)
+
             quantise(pw_codes, pw_scales, pw_grouped)
             quantise(p1_codes, p1_scales, p1_grouped)
 
@@ -164,23 +153,13 @@ def tile_dssattention_pa_t_kernel(tc, wv, x, dw_w, dw_b, pw_w, pw_b, p_w1, out):
                 a_planes[c] = planes
             for i in range(2):
                 t = 2 * h + i
-                if h == 0:
-                    nc.scalar.activation(
-                        out=a_planes[c][:, t, :],
-                        in_=wv_t[c, h][:, i, :],
-                        func=IDENTITY,
-                        scale=dw[:, t, 0:1],
-                        bias=dw[:, t, 1:2],
-                    )
-                else:
-                    nc.vector.tensor_scalar(
-                        out=a_planes[c][:, t, :],
-                        in0=wv_t[c, h][:, i, :],
-                        scalar1=dw[:, t, 0:1],
-                        scalar2=dw[:, t, 1:2],
-                        op0=MULT,
-                        op1=ADD,
-                    )
+                nc.scalar.activation(
+                    out=a_planes[c][:, t, :],
+                    in_=wv_t[c, h][:, i, :],
+                    func=IDENTITY,
+                    scale=per_channel[:, t, 0:1],
+                    bias=per_channel[:, t, 1:2],
+                )
 
         def group_a(c):
             if not live(c):
@@ -223,18 +202,17 @@ def tile_dssattention_pa_t_kernel(tc, wv, x, dw_w, dw_b, pw_w, pw_b, p_w1, out):
                 in_=dyn[c, j][:],
                 func=IDENTITY,
                 scale=1.0,
-                bias=pw_bias[:, j // 2, j % 2 : j % 2 + 1],
+                bias=per_channel[:, j, 2:3],
             )
 
         def transpose_x(c, h):
             if not live(c):
                 return
-            bank = psum_x.tile([P, 2, HALF], F32, tag="x_t")
-            words = x_rows[c][:].bitcast(F32)
-            for u in range(2):
+            bank = psum_x.tile([P, PACK, HALF], BF16, tag="x_t")
+            for t in range(PACK):
                 for i in range(2):
                     nc.tensor.transpose(
-                        bank[:, u, i * P : (i + 1) * P], words[:, 2 * h + i, u * P : (u + 1) * P], ident_f32[:]
+                        bank[:, t, i * P : (i + 1) * P], x_rows[c][:, 2 * h + i, t * P : (t + 1) * P], ident_bf16[:]
                     )
             x_t[c, h] = bank
 
@@ -246,9 +224,9 @@ def tile_dssattention_pa_t_kernel(tc, wv, x, dw_w, dw_b, pw_w, pw_b, p_w1, out):
                 y_grouped[c] = grouped
             tokens = slice(h * HALF, (h + 1) * HALF)
             nc.vector.tensor_tensor(
-                out=y_grouped[c][:, tokens, :].rearrange("p w (u e) -> p w u e", u=2),
-                in0=x_t[c, h][:].bitcast(BF16).rearrange("p u (w e) -> p w u e", e=2),
-                in1=dyn_biased[c][:, :, tokens].rearrange("p (u e) w -> p w u e", u=2),
+                out=y_grouped[c][:, tokens, :].rearrange("p (c i) t -> p c t i", i=4),
+                in0=x_t[c, h][:].rearrange("p t (c i) -> p c t i", i=4),
+                in1=dyn_biased[c][:, :, tokens].rearrange("p t (c i) -> p c t i", i=4),
                 op=ADD,
             )
 

@@ -10,6 +10,7 @@ U8 = mybir.dt.uint8
 FP8X4 = mybir.dt.float8_e4m3fn_x4
 IDENTITY = mybir.ActivationFunctionType.Identity
 ADD = mybir.AluOpType.add
+MULT = mybir.AluOpType.mult
 
 P = 128
 PACK = 4
@@ -165,7 +166,16 @@ def tile_dssattention_pa_t_kernel(tc, wv, x, dw_w, dw_b, pw_w, pw_b, p_w1, out):
             if not live(c):
                 return
             grouped = work.tile([P, CHUNK, PACK], BF16, tag="a_grouped", align_bytes=64)
-            group_planes(grouped, a_planes[c])
+            for h in range(2):
+                tokens = slice(h * HALF, (h + 1) * HALF)
+                nc.gpsimd.tensor_scalar(
+                    out=grouped[:, tokens, :],
+                    in0=a_planes[c][:, :, tokens].rearrange("p t w -> p w t"),
+                    scalar1=1.0,
+                    scalar2=0.0,
+                    op0=MULT,
+                    op1=ADD,
+                )
             a_grouped[c] = grouped
 
         def quantise_a(c):
@@ -259,7 +269,7 @@ def tile_dssattention_pa_t_kernel(tc, wv, x, dw_w, dw_b, pw_w, pw_b, p_w1, out):
                 return
             result = work.tile([P, TILES, RANK], F32, tag="result")
             nc.scalar.copy(out=result[:], in_=out_acc[c][:])
-            nc.gpsimd.dma_start(out=out_chunks[c], in_=result[:].rearrange("p q r -> p (q r)"))
+            nc.sync.dma_start(out=out_chunks[c], in_=result[:].rearrange("p q r -> p (q r)"))
 
 
         def step(n):

@@ -8,7 +8,6 @@ BF16 = mybir.dt.bfloat16
 U32 = mybir.dt.uint32
 U8 = mybir.dt.uint8
 FP8X4 = mybir.dt.float8_e4m3fn_x4
-IDENTITY = mybir.ActivationFunctionType.Identity
 ADD = mybir.AluOpType.add
 MULT = mybir.AluOpType.mult
 
@@ -38,18 +37,16 @@ def tile_dssattention_pa_t_kernel(tc, wv, x, dw_w, dw_b, pw_w, pw_b, p_w1, out):
         work = stack.enter_context(tc.tile_pool(name="work", bufs=3))
         psum_wv = stack.enter_context(tc.psum_pool(name="psum_wv", bufs=2))
         psum_x = stack.enter_context(tc.psum_pool(name="psum_x", bufs=2))
-        psum_dyn = stack.enter_context(tc.psum_pool(name="psum_dyn", bufs=2))
-        psum_out = stack.enter_context(tc.psum_pool(name="psum_out", bufs=2))
+        psum_dyn = stack.enter_context(tc.psum_pool(name="psum_dyn", bufs=3))
+        psum_out = stack.enter_context(tc.psum_pool(name="psum_out", bufs=1))
         stack.enter_context(tc.manual_schedule())
 
-        wv_rows, x_rows, wv_t, x_t = {}, {}, {}, {}
-        a_planes, a_codes, a_scales = {}, {}, {}
-        dyn, dyn_biased, y_grouped, y_codes, y_scales, out_acc = {}, {}, {}, {}, {}, {}
-        a_grouped = {}
+        wv_rows, x_rows, wv_t, x_t, x_words = {}, {}, {}, {}, {}
+        a_planes, a_grouped, a_codes, a_scales = {}, {}, {}, {}
+        dyn, y_planes, y_grouped, y_codes, y_scales, out_acc = {}, {}, {}, {}, {}, {}
 
         def live(c):
             return 0 <= c < N_CHUNKS
-
 
         def transpose_channel_planes(bank, rows, h):
             for i in range(2):
@@ -59,19 +56,12 @@ def tile_dssattention_pa_t_kernel(tc, wv, x, dw_w, dw_b, pw_w, pw_b, p_w1, out):
                         bank[:, i, q * P : (q + 1) * P], rows[:, q, t * P : (t + 1) * P], ident_bf16[:]
                     )
 
-        def group_planes(grouped, planes):
-            nc.vector.tensor_copy(
-                out=grouped[:].rearrange("p (c i) t -> p c t i", i=4),
-                in_=planes[:].rearrange("p t (c i) -> p c t i", i=4),
-            )
-
         def quantise(codes, scales, grouped):
             nc.vector.quantize_mx(
                 out=codes[:].bitcast(FP8X4),
                 scales=scales[:],
                 in_=grouped[:].rearrange("p w t -> p (w t)"),
             )
-
 
         def load_wv(c):
             if not live(c):
@@ -90,6 +80,8 @@ def tile_dssattention_pa_t_kernel(tc, wv, x, dw_w, dw_b, pw_w, pw_b, p_w1, out):
 
         ident_bf16 = const.tile([P, P], BF16)
         masks.make_identity(nc, ident_bf16[:])
+        ident_f32 = const.tile([P, P], F32)
+        masks.make_identity(nc, ident_f32[:])
 
         vectors = const.tile([P, CHANNELS], BF16)
         nc.vector.memset(vectors[:], 0.0)
@@ -98,7 +90,11 @@ def tile_dssattention_pa_t_kernel(tc, wv, x, dw_w, dw_b, pw_w, pw_b, p_w1, out):
 
         load_wv(0)
         pw_rows = const.tile([P, PACK, CHANNELS], BF16)
-        nc.sync.dma_start(out=pw_rows[:], in_=pw_w.rearrange("(j m) k -> m j k", m=P))
+        for u in range(2):
+            nc.sync.dma_start(
+                out=pw_rows[:, 2 * u : 2 * u + 2, :],
+                in_=pw_w[256 * u : 256 * (u + 1), :].rearrange("(m e) k -> m e k", e=2),
+            )
         load_wv(1)
         p1_rows = const.tile([P, CHANNELS], BF16)
         nc.sync.dma_start(out=p1_rows[:], in_=p_w1)
@@ -108,9 +104,19 @@ def tile_dssattention_pa_t_kernel(tc, wv, x, dw_w, dw_b, pw_w, pw_b, p_w1, out):
             nc.tensor.transpose(
                 vectors_t[:, 0, t * P : (t + 1) * P], vectors[:, t * P : (t + 1) * P], ident_bf16[:]
             )
-        per_channel = const.tile([P, PACK, 3], F32)
+        affine_consts = const.tile([P, PACK, 2], F32)
         nc.vector.tensor_copy(
-            out=per_channel[:], in_=vectors_t[:, 0, :].rearrange("p (t r) -> p t r", t=PACK)[:, :, 0:3]
+            out=affine_consts[:], in_=vectors_t[:, 0, :].rearrange("p (t r) -> p t r", t=PACK)[:, :, 0:2]
+        )
+        vector_words_t = psum_dyn.tile([P, 2, P], F32, tag="dyn")
+        for u in range(2):
+            nc.tensor.transpose(
+                vector_words_t[:, u, :], vectors[:].bitcast(F32)[:, u * P : (u + 1) * P], ident_f32[:]
+            )
+        bias_y = const.tile([P, 2, 2], F32)
+        nc.vector.tensor_copy(
+            out=bias_y[:],
+            in_=vector_words_t[:].bitcast(BF16).rearrange("p u (r e) -> p u r e", e=2)[:, :, 2, :],
         )
 
         p1_codes = const.tile([P, RANK], U32, align_bytes=64)
@@ -125,15 +131,16 @@ def tile_dssattention_pa_t_kernel(tc, wv, x, dw_w, dw_b, pw_w, pw_b, p_w1, out):
                 transpose_channel_planes(bank, pw_rows, h)
                 nc.vector.tensor_copy(out=pw_planes[:, 2 * h : 2 * h + 2, :], in_=bank[:])
             pw_grouped = const.tile([P, CHUNK, PACK], BF16, align_bytes=64)
-            group_planes(pw_grouped, pw_planes)
+            nc.vector.tensor_copy(out=pw_grouped[:], in_=pw_planes[:].rearrange("p t w -> p w t"))
 
-            p1_t = psum_out.tile([P, PACK, RANK], BF16, tag="out_acc")
-            for t in range(PACK):
-                nc.tensor.transpose(p1_t[:, t, :], p1_rows[:, t * P : (t + 1) * P], ident_bf16[:])
-            p1_planes = const.tile([P, PACK, RANK], BF16)
-            nc.vector.tensor_copy(out=p1_planes[:], in_=p1_t[:])
+            p1_t = psum_out.tile([P, 2, RANK], F32, tag="out_acc")
+            for u in range(2):
+                nc.tensor.transpose(p1_t[:, u, :], p1_rows[:].bitcast(F32)[:, u * P : (u + 1) * P], ident_f32[:])
             p1_grouped = const.tile([P, RANK, PACK], BF16, align_bytes=64)
-            group_planes(p1_grouped, p1_planes)
+            nc.vector.tensor_copy(
+                out=p1_grouped[:].rearrange("p r t -> p (r t)").bitcast(F32).rearrange("p (r u) -> p r u", u=2),
+                in_=p1_t[:].rearrange("p u r -> p r u"),
+            )
 
             quantise(pw_codes, pw_scales, pw_grouped)
             quantise(p1_codes, p1_scales, p1_grouped)
@@ -154,29 +161,25 @@ def tile_dssattention_pa_t_kernel(tc, wv, x, dw_w, dw_b, pw_w, pw_b, p_w1, out):
                 a_planes[c] = planes
             for i in range(2):
                 t = 2 * h + i
-                nc.scalar.activation(
+                nc.vector.tensor_scalar(
                     out=a_planes[c][:, t, :],
-                    in_=wv_t[c, h][:, i, :],
-                    func=IDENTITY,
-                    scale=per_channel[:, t, 0:1],
-                    bias=per_channel[:, t, 1:2],
-                )
-
-        def group_a(c):
-            if not live(c):
-                return
-            grouped = work.tile([P, CHUNK, PACK], BF16, tag="a_grouped", align_bytes=64)
-            for h in range(2):
-                tokens = slice(h * HALF, (h + 1) * HALF)
-                nc.gpsimd.tensor_scalar(
-                    out=grouped[:, tokens, :],
-                    in0=a_planes[c][:, :, tokens].rearrange("p t w -> p w t"),
-                    scalar1=1.0,
-                    scalar2=0.0,
+                    in0=wv_t[c, h][:, i, :],
+                    scalar1=affine_consts[:, t, 0:1],
+                    scalar2=affine_consts[:, t, 1:2],
                     op0=MULT,
                     op1=ADD,
                 )
-            a_grouped[c] = grouped
+
+        def group_a(c, h):
+            if not live(c):
+                return
+            if h == 0:
+                grouped = work.tile([P, CHUNK, PACK], BF16, tag="a_grouped", align_bytes=64)
+                a_grouped[c] = grouped
+            tokens = slice(h * HALF, (h + 1) * HALF)
+            nc.scalar.copy(
+                out=a_grouped[c][:, tokens, :], in_=a_planes[c][:, :, tokens].rearrange("p t w -> p w t")
+            )
 
         def quantise_a(c):
             if not live(c):
@@ -201,44 +204,57 @@ def tile_dssattention_pa_t_kernel(tc, wv, x, dw_w, dw_b, pw_w, pw_b, p_w1, out):
             )
             dyn[c, j] = acc
 
-        def add_bias(c, j):
+        def transpose_x(c, u):
+            if not live(c):
+                return
+            bank = psum_x.tile([P, CHUNK], F32, tag="x_t")
+            for q in range(TILES):
+                nc.tensor.transpose(
+                    bank[:, q * P : (q + 1) * P],
+                    x_rows[c][:].bitcast(F32)[:, q, u * P : (u + 1) * P],
+                    ident_f32[:],
+                )
+            x_t[c, u] = bank
+
+        def copy_x(c, u):
+            if not live(c):
+                return
+            if u == 0:
+                words = work.tile([P, 2, CHUNK], F32, tag="x_words")
+                x_words[c] = words
+            nc.scalar.copy(out=x_words[c][:, u, :], in_=x_t[c, u][:])
+
+        def add_x(c, j):
             if not live(c):
                 return
             if j == 0:
-                biased = work.tile([P, PACK, CHUNK], F32, tag="dyn_biased")
-                dyn_biased[c] = biased
-            nc.scalar.activation(
-                out=dyn_biased[c][:, j, :],
-                in_=dyn[c, j][:],
-                func=IDENTITY,
-                scale=1.0,
-                bias=per_channel[:, j, 2:3],
+                planes = work.tile([P, PACK, CHUNK], BF16, tag="y_planes")
+                y_planes[c] = planes
+            u, e = divmod(j, 2)
+            nc.vector.scalar_tensor_tensor(
+                out=y_planes[c][:, j, :],
+                in0=dyn[c, j][:],
+                scalar=bias_y[:, u, e : e + 1],
+                in1=x_words[c][:].bitcast(BF16).rearrange("p u (w e) -> p u w e", e=2)[:, u, :, e],
+                op0=ADD,
+                op1=ADD,
             )
 
-        def transpose_x(c, h):
+        def group_y(c):
             if not live(c):
                 return
-            bank = psum_x.tile([P, PACK, HALF], BF16, tag="x_t")
-            for t in range(PACK):
-                for i in range(2):
-                    nc.tensor.transpose(
-                        bank[:, t, i * P : (i + 1) * P], x_rows[c][:, 2 * h + i, t * P : (t + 1) * P], ident_bf16[:]
-                    )
-            x_t[c, h] = bank
-
-        def add_x(c, h):
-            if not live(c):
-                return
-            if h == 0:
-                grouped = work.tile([P, CHUNK, PACK], BF16, tag="y_grouped", align_bytes=64)
-                y_grouped[c] = grouped
-            tokens = slice(h * HALF, (h + 1) * HALF)
-            nc.vector.tensor_tensor(
-                out=y_grouped[c][:, tokens, :].rearrange("p (c i) t -> p c t i", i=4),
-                in0=x_t[c, h][:].rearrange("p t (c i) -> p c t i", i=4),
-                in1=dyn_biased[c][:, :, tokens].rearrange("p t (c i) -> p c t i", i=4),
-                op=ADD,
-            )
+            grouped = work.tile([P, CHUNK, PACK], BF16, tag="y_grouped", align_bytes=64)
+            for h in range(2):
+                tokens = slice(h * HALF, (h + 1) * HALF)
+                nc.gpsimd.tensor_scalar(
+                    out=grouped[:, tokens, :],
+                    in0=y_planes[c][:, :, tokens].rearrange("p t w -> p w t"),
+                    scalar1=1.0,
+                    scalar2=0.0,
+                    op0=MULT,
+                    op1=ADD,
+                )
+            y_grouped[c] = grouped
 
         def quantise_y(c):
             if not live(c):
@@ -274,27 +290,29 @@ def tile_dssattention_pa_t_kernel(tc, wv, x, dw_w, dw_b, pw_w, pw_b, p_w1, out):
 
         def step(n):
             load_wv(n + 3)
-            load_x(n)
+            load_x(n + 1)
 
+            copy_x(n - 2, 1)
+            group_y(n - 3)
             first_matmul(n - 2, 0)
             first_matmul(n - 2, 1)
             affine(n, 0)
-            add_x(n - 3, 0)
             transpose_wv(n, 1)
-            transpose_x(n - 2, 0)
-            add_bias(n - 2, 0)
-            add_bias(n - 2, 1)
-            group_a(n - 1)
+            transpose_x(n - 1, 0)
+            group_a(n - 1, 0)
+            add_x(n - 2, 0)
+            add_x(n - 2, 1)
 
             first_matmul(n - 2, 2)
             first_matmul(n - 2, 3)
             second_matmul(n - 4)
             affine(n, 1)
-            add_x(n - 3, 1)
             transpose_wv(n + 1, 0)
-            transpose_x(n - 2, 1)
-            add_bias(n - 2, 2)
-            add_bias(n - 2, 3)
+            transpose_x(n - 1, 1)
+            group_a(n - 1, 1)
+            copy_x(n - 1, 0)
+            add_x(n - 2, 2)
+            add_x(n - 2, 3)
             quantise_a(n - 1)
             quantise_y(n - 3)
             store(n - 4)

@@ -20,6 +20,7 @@ CHUNK = 512
 TILES = CHUNK // P
 HALF = CHUNK // 2
 N_CHUNKS = TOKENS // CHUNK
+GPSIMD_SHARE = 384
 
 FLOPS = 2 * TOKENS * CHANNELS * CHANNELS + 2 * TOKENS * CHANNELS * RANK
 
@@ -34,7 +35,7 @@ def tile_dssattention_pa_t_kernel(tc, wv, x, dw_w, dw_b, pw_w, pw_b, p_w1, out):
     with ExitStack() as stack:
         const = stack.enter_context(tc.tile_pool(name="const", bufs=1))
         loads = stack.enter_context(tc.tile_pool(name="loads", bufs=4))
-        work = stack.enter_context(tc.tile_pool(name="work", bufs=3))
+        work = stack.enter_context(tc.tile_pool(name="work", bufs=4))
         psum_wv = stack.enter_context(tc.psum_pool(name="psum_wv", bufs=2))
         psum_x = stack.enter_context(tc.psum_pool(name="psum_x", bufs=2))
         psum_dyn = stack.enter_context(tc.psum_pool(name="psum_dyn", bufs=3))
@@ -124,24 +125,34 @@ def tile_dssattention_pa_t_kernel(tc, wv, x, dw_w, dw_b, pw_w, pw_b, p_w1, out):
         pw_codes = const.tile([P, CHUNK], U32, align_bytes=64)
         pw_scales = const.tile([P, CHUNK], U8, align_bytes=64)
 
-        def prepare_weights():
-            pw_planes = const.tile([P, PACK, CHUNK], BF16)
+        pw_planes = const.tile([P, PACK, CHUNK], BF16)
+        pw_grouped = const.tile([P, CHUNK, PACK], BF16, align_bytes=64)
+        p1_grouped = const.tile([P, RANK, PACK], BF16, align_bytes=64)
+
+        def lay_out_weights():
             for h in range(2):
                 bank = psum_dyn.tile([P, 2, CHUNK], BF16, tag="dyn")
                 transpose_channel_planes(bank, pw_rows, h)
-                nc.vector.tensor_copy(out=pw_planes[:, 2 * h : 2 * h + 2, :], in_=bank[:])
-            pw_grouped = const.tile([P, CHUNK, PACK], BF16, align_bytes=64)
-            nc.vector.tensor_copy(out=pw_grouped[:], in_=pw_planes[:].rearrange("p t w -> p w t"))
-
+                nc.scalar.copy(out=pw_planes[:, 2 * h : 2 * h + 2, :], in_=bank[:])
+            for h in range(2):
+                rows = slice(h * HALF, (h + 1) * HALF)
+                nc.gpsimd.tensor_scalar(
+                    out=pw_grouped[:, rows, :],
+                    in0=pw_planes[:, :, rows].rearrange("p t w -> p w t"),
+                    scalar1=1.0,
+                    scalar2=0.0,
+                    op0=MULT,
+                    op1=ADD,
+                )
             p1_t = psum_out.tile([P, 2, RANK], F32, tag="out_acc")
             for u in range(2):
                 nc.tensor.transpose(p1_t[:, u, :], p1_rows[:].bitcast(F32)[:, u * P : (u + 1) * P], ident_f32[:])
-            p1_grouped = const.tile([P, RANK, PACK], BF16, align_bytes=64)
-            nc.vector.tensor_copy(
+            nc.scalar.copy(
                 out=p1_grouped[:].rearrange("p r t -> p (r t)").bitcast(F32).rearrange("p (r u) -> p r u", u=2),
                 in_=p1_t[:].rearrange("p u r -> p r u"),
             )
 
+        def quantise_weights():
             quantise(pw_codes, pw_scales, pw_grouped)
             quantise(p1_codes, p1_scales, p1_grouped)
 
@@ -178,7 +189,8 @@ def tile_dssattention_pa_t_kernel(tc, wv, x, dw_w, dw_b, pw_w, pw_b, p_w1, out):
                 a_grouped[c] = grouped
             tokens = slice(h * HALF, (h + 1) * HALF)
             nc.scalar.copy(
-                out=a_grouped[c][:, tokens, :], in_=a_planes[c][:, :, tokens].rearrange("p t w -> p w t")
+                out=a_grouped[c][:, tokens, :].rearrange("p (c i) t -> p c t i", i=4),
+                in_=a_planes[c][:, :, tokens].rearrange("p t (c i) -> p c t i", i=4),
             )
 
         def quantise_a(c):
@@ -244,8 +256,13 @@ def tile_dssattention_pa_t_kernel(tc, wv, x, dw_w, dw_b, pw_w, pw_b, p_w1, out):
             if not live(c):
                 return
             grouped = work.tile([P, CHUNK, PACK], BF16, tag="y_grouped", align_bytes=64)
+            tokens = slice(GPSIMD_SHARE, CHUNK)
+            nc.scalar.copy(
+                out=grouped[:, tokens, :].rearrange("p (c i) t -> p c t i", i=4),
+                in_=y_planes[c][:, :, tokens].rearrange("p t (c i) -> p c t i", i=4),
+            )
             for h in range(2):
-                tokens = slice(h * HALF, (h + 1) * HALF)
+                tokens = slice(h * GPSIMD_SHARE // 2, (h + 1) * GPSIMD_SHARE // 2)
                 nc.gpsimd.tensor_scalar(
                     out=grouped[:, tokens, :],
                     in0=y_planes[c][:, :, tokens].rearrange("p t w -> p w t"),
@@ -290,35 +307,38 @@ def tile_dssattention_pa_t_kernel(tc, wv, x, dw_w, dw_b, pw_w, pw_b, p_w1, out):
 
         def step(n):
             load_wv(n + 3)
-            load_x(n + 1)
+            load_x(n)
 
-            copy_x(n - 2, 1)
-            group_y(n - 3)
-            first_matmul(n - 2, 0)
-            first_matmul(n - 2, 1)
+            group_y(n - 4)
+            copy_x(n - 3, 1)
+            first_matmul(n - 3, 0)
+            first_matmul(n - 3, 1)
             affine(n, 0)
             transpose_wv(n, 1)
-            transpose_x(n - 1, 0)
+            transpose_x(n - 2, 0)
             group_a(n - 1, 0)
-            add_x(n - 2, 0)
-            add_x(n - 2, 1)
+            add_x(n - 3, 0)
+            add_x(n - 3, 1)
 
-            first_matmul(n - 2, 2)
-            first_matmul(n - 2, 3)
-            second_matmul(n - 4)
+            first_matmul(n - 3, 2)
+            first_matmul(n - 3, 3)
+            second_matmul(n - 5)
             affine(n, 1)
             transpose_wv(n + 1, 0)
-            transpose_x(n - 1, 1)
+            transpose_x(n - 2, 1)
             group_a(n - 1, 1)
-            copy_x(n - 1, 0)
-            add_x(n - 2, 2)
-            add_x(n - 2, 3)
-            quantise_a(n - 1)
-            quantise_y(n - 3)
-            store(n - 4)
+            copy_x(n - 2, 0)
+            add_x(n - 3, 2)
+            add_x(n - 3, 3)
+            quantise_a(n - 2)
+            quantise_y(n - 4)
+            store(n - 5)
 
         step(-1)
         step(0)
-        prepare_weights()
-        for n in range(1, N_CHUNKS + 4):
+        lay_out_weights()
+        step(1)
+        quantise_weights()
+        step(2)
+        for n in range(3, N_CHUNKS + 5):
             step(n)

@@ -256,6 +256,15 @@ def tile_dssattention_pa_t_kernel(tc, wv, x, dw_w, dw_b, pw_w, pw_b, p_w1, out):
             if not live(c):
                 return
             grouped = work.tile([P, CHUNK, PACK], BF16, tag="y_grouped", align_bytes=64)
+            y_grouped[c] = grouped
+            if c == N_CHUNKS - 1:
+                for h in range(2):
+                    tokens = slice(h * HALF, (h + 1) * HALF)
+                    nc.vector.tensor_copy(
+                        out=grouped[:, tokens, :].rearrange("p (c i) t -> p c t i", i=4),
+                        in_=y_planes[c][:, :, tokens].rearrange("p t (c i) -> p c t i", i=4),
+                    )
+                return
             tokens = slice(GPSIMD_SHARE, CHUNK)
             nc.scalar.copy(
                 out=grouped[:, tokens, :].rearrange("p (c i) t -> p c t i", i=4),
@@ -271,15 +280,23 @@ def tile_dssattention_pa_t_kernel(tc, wv, x, dw_w, dw_b, pw_w, pw_b, p_w1, out):
                     op0=MULT,
                     op1=ADD,
                 )
-            y_grouped[c] = grouped
 
         def quantise_y(c):
             if not live(c):
                 return
             codes = work.tile([P, CHUNK], U32, tag="y_codes", align_bytes=64)
             scales = work.tile([P, CHUNK], U8, tag="y_scales", align_bytes=64)
-            quantise(codes, scales, y_grouped[c])
             y_codes[c], y_scales[c] = codes, scales
+            if c == N_CHUNKS - 1:
+                for h in range(2):
+                    tokens = slice(h * HALF, (h + 1) * HALF)
+                    nc.vector.quantize_mx(
+                        out=codes[:, tokens].bitcast(FP8X4),
+                        scales=scales[:, tokens],
+                        in_=y_grouped[c][:, tokens, :].rearrange("p w t -> p (w t)"),
+                    )
+                return
+            quantise(codes, scales, y_grouped[c])
 
         def second_matmul(c):
             if not live(c):
@@ -301,8 +318,15 @@ def tile_dssattention_pa_t_kernel(tc, wv, x, dw_w, dw_b, pw_w, pw_b, p_w1, out):
             if not live(c):
                 return
             result = work.tile([P, TILES, RANK], F32, tag="result")
-            nc.scalar.copy(out=result[:], in_=out_acc[c][:])
-            nc.sync.dma_start(out=out_chunks[c], in_=result[:].rearrange("p q r -> p (q r)"))
+            pieces = 2 if c == N_CHUNKS - 1 else 1
+            width = TILES // pieces
+            for i in range(pieces):
+                tiles = slice(i * width, (i + 1) * width)
+                nc.scalar.copy(out=result[:, tiles, :], in_=out_acc[c][:, tiles, :])
+                nc.sync.dma_start(
+                    out=out_chunks[c][:, i * width * RANK : (i + 1) * width * RANK],
+                    in_=result[:, tiles, :].rearrange("p q r -> p (q r)"),
+                )
 
 
         def step(n):
@@ -338,7 +362,7 @@ def tile_dssattention_pa_t_kernel(tc, wv, x, dw_w, dw_b, pw_w, pw_b, p_w1, out):
         step(0)
         lay_out_weights()
         step(1)
-        quantise_weights()
         step(2)
+        quantise_weights()
         for n in range(3, N_CHUNKS + 5):
             step(n)

@@ -8,6 +8,7 @@ BF16 = mybir.dt.bfloat16
 U32 = mybir.dt.uint32
 U8 = mybir.dt.uint8
 FP8X4 = mybir.dt.float8_e4m3fn_x4
+IDENTITY = mybir.ActivationFunctionType.Identity
 ADD = mybir.AluOpType.add
 MULT = mybir.AluOpType.mult
 
@@ -20,7 +21,7 @@ CHUNK = 512
 TILES = CHUNK // P
 HALF = CHUNK // 2
 N_CHUNKS = TOKENS // CHUNK
-GPSIMD_SHARE = 384
+SCALAR_AFFINE_EVERY = 3
 
 FLOPS = 2 * TOKENS * CHANNELS * CHANNELS + 2 * TOKENS * CHANNELS * RANK
 
@@ -172,14 +173,23 @@ def tile_dssattention_pa_t_kernel(tc, wv, x, dw_w, dw_b, pw_w, pw_b, p_w1, out):
                 a_planes[c] = planes
             for i in range(2):
                 t = 2 * h + i
-                nc.vector.tensor_scalar(
-                    out=a_planes[c][:, t, :],
-                    in0=wv_t[c, h][:, i, :],
-                    scalar1=affine_consts[:, t, 0:1],
-                    scalar2=affine_consts[:, t, 1:2],
-                    op0=MULT,
-                    op1=ADD,
-                )
+                if h == 1 and c % SCALAR_AFFINE_EVERY == SCALAR_AFFINE_EVERY - 1:
+                    nc.scalar.activation(
+                        out=a_planes[c][:, t, :],
+                        in_=wv_t[c, h][:, i, :],
+                        func=IDENTITY,
+                        scale=affine_consts[:, t, 0:1],
+                        bias=affine_consts[:, t, 1:2],
+                    )
+                else:
+                    nc.vector.tensor_scalar(
+                        out=a_planes[c][:, t, :],
+                        in0=wv_t[c, h][:, i, :],
+                        scalar1=affine_consts[:, t, 0:1],
+                        scalar2=affine_consts[:, t, 1:2],
+                        op0=MULT,
+                        op1=ADD,
+                    )
 
         def group_a(c, h):
             if not live(c):
@@ -265,21 +275,14 @@ def tile_dssattention_pa_t_kernel(tc, wv, x, dw_w, dw_b, pw_w, pw_b, p_w1, out):
                         in_=y_planes[c][:, :, tokens].rearrange("p t (c i) -> p c t i", i=4),
                     )
                 return
-            tokens = slice(GPSIMD_SHARE, CHUNK)
-            nc.scalar.copy(
-                out=grouped[:, tokens, :].rearrange("p (c i) t -> p c t i", i=4),
-                in_=y_planes[c][:, :, tokens].rearrange("p t (c i) -> p c t i", i=4),
+            nc.gpsimd.tensor_scalar(
+                out=grouped[:],
+                in0=y_planes[c][:].rearrange("p t w -> p w t"),
+                scalar1=1.0,
+                scalar2=0.0,
+                op0=MULT,
+                op1=ADD,
             )
-            for h in range(2):
-                tokens = slice(h * GPSIMD_SHARE // 2, (h + 1) * GPSIMD_SHARE // 2)
-                nc.gpsimd.tensor_scalar(
-                    out=grouped[:, tokens, :],
-                    in0=y_planes[c][:, :, tokens].rearrange("p t w -> p w t"),
-                    scalar1=1.0,
-                    scalar2=0.0,
-                    op0=MULT,
-                    op1=ADD,
-                )
 
         def quantise_y(c):
             if not live(c):

@@ -21,7 +21,8 @@ CHUNK = 512
 TILES = CHUNK // P
 HALF = CHUNK // 2
 N_CHUNKS = TOKENS // CHUNK
-SCALAR_AFFINE_EVERY = 3
+RUN = 4
+LAST = N_CHUNKS - 1
 
 FLOPS = 2 * TOKENS * CHANNELS * CHANNELS + 2 * TOKENS * CHANNELS * RANK
 
@@ -43,9 +44,9 @@ def tile_dssattention_pa_t_kernel(tc, wv, x, dw_w, dw_b, pw_w, pw_b, p_w1, out):
         psum_out = stack.enter_context(tc.psum_pool(name="psum_out", bufs=1))
         stack.enter_context(tc.manual_schedule())
 
-        wv_rows, x_rows, wv_t, x_t, x_words = {}, {}, {}, {}, {}
+        wv_rows, x_rows, wv_t, x_t, x_biased = {}, {}, {}, {}, {}
         a_planes, a_grouped, a_codes, a_scales = {}, {}, {}, {}
-        dyn, y_planes, y_grouped, y_codes, y_scales, out_acc = {}, {}, {}, {}, {}, {}
+        dyn, y_grouped, y_codes, y_scales, out_acc = {}, {}, {}, {}, {}
 
         def live(c):
             return 0 <= c < N_CHUNKS
@@ -135,16 +136,7 @@ def tile_dssattention_pa_t_kernel(tc, wv, x, dw_w, dw_b, pw_w, pw_b, p_w1, out):
                 bank = psum_dyn.tile([P, 2, CHUNK], BF16, tag="dyn")
                 transpose_channel_planes(bank, pw_rows, h)
                 nc.scalar.copy(out=pw_planes[:, 2 * h : 2 * h + 2, :], in_=bank[:])
-            for h in range(2):
-                rows = slice(h * HALF, (h + 1) * HALF)
-                nc.gpsimd.tensor_scalar(
-                    out=pw_grouped[:, rows, :],
-                    in0=pw_planes[:, :, rows].rearrange("p t w -> p w t"),
-                    scalar1=1.0,
-                    scalar2=0.0,
-                    op0=MULT,
-                    op1=ADD,
-                )
+            nc.vector.tensor_copy(out=pw_grouped[:], in_=pw_planes[:].rearrange("p t w -> p w t"))
             p1_t = psum_out.tile([P, 2, RANK], F32, tag="out_acc")
             for u in range(2):
                 nc.tensor.transpose(p1_t[:, u, :], p1_rows[:].bitcast(F32)[:, u * P : (u + 1) * P], ident_f32[:])
@@ -173,15 +165,7 @@ def tile_dssattention_pa_t_kernel(tc, wv, x, dw_w, dw_b, pw_w, pw_b, p_w1, out):
                 a_planes[c] = planes
             for i in range(2):
                 t = 2 * h + i
-                if h == 1 and c % SCALAR_AFFINE_EVERY == SCALAR_AFFINE_EVERY - 1:
-                    nc.scalar.activation(
-                        out=a_planes[c][:, t, :],
-                        in_=wv_t[c, h][:, i, :],
-                        func=IDENTITY,
-                        scale=affine_consts[:, t, 0:1],
-                        bias=affine_consts[:, t, 1:2],
-                    )
-                else:
+                if h == 0:
                     nc.vector.tensor_scalar(
                         out=a_planes[c][:, t, :],
                         in0=wv_t[c, h][:, i, :],
@@ -190,18 +174,28 @@ def tile_dssattention_pa_t_kernel(tc, wv, x, dw_w, dw_b, pw_w, pw_b, p_w1, out):
                         op0=MULT,
                         op1=ADD,
                     )
+                else:
+                    nc.scalar.activation(
+                        out=a_planes[c][:, t, :],
+                        in_=wv_t[c, h][:, i, :],
+                        func=IDENTITY,
+                        scale=affine_consts[:, t, 0:1],
+                        bias=affine_consts[:, t, 1:2],
+                    )
 
-        def group_a(c, h):
+        def group_a(c):
             if not live(c):
                 return
-            if h == 0:
-                grouped = work.tile([P, CHUNK, PACK], BF16, tag="a_grouped", align_bytes=64)
-                a_grouped[c] = grouped
-            tokens = slice(h * HALF, (h + 1) * HALF)
-            nc.scalar.copy(
-                out=a_grouped[c][:, tokens, :].rearrange("p (c i) t -> p c t i", i=4),
-                in_=a_planes[c][:, :, tokens].rearrange("p t (c i) -> p c t i", i=4),
+            grouped = work.tile([P, CHUNK, PACK], BF16, tag="a_grouped", bufs=1, align_bytes=64)
+            nc.gpsimd.tensor_scalar(
+                out=grouped[:],
+                in0=a_planes[c][:].rearrange("p t w -> p w t"),
+                scalar1=1.0,
+                scalar2=0.0,
+                op0=MULT,
+                op1=ADD,
             )
+            a_grouped[c] = grouped
 
         def quantise_a(c):
             if not live(c):
@@ -211,20 +205,21 @@ def tile_dssattention_pa_t_kernel(tc, wv, x, dw_w, dw_b, pw_w, pw_b, p_w1, out):
             quantise(codes, scales, a_grouped[c])
             a_codes[c], a_scales[c] = codes, scales
 
-        def first_matmul(c, j):
+        def first_matmul(c, q):
             if not live(c):
                 return
-            acc = psum_dyn.tile([P, CHUNK], F32, tag="dyn")
-            nc.tensor.matmul_mx(
-                out=acc[:],
-                lhsT=pw_codes[:, j * P : (j + 1) * P].bitcast(FP8X4),
-                lhsT_scale=pw_scales[:, j * P : (j + 1) * P],
-                rhs=a_codes[c][:].bitcast(FP8X4),
-                rhs_scale=a_scales[c][:],
-                start=True,
-                stop=True,
-            )
-            dyn[c, j] = acc
+            acc = psum_dyn.tile([P, PACK, P], F32, tag="dyn")
+            for j in range(PACK):
+                nc.tensor.matmul_mx(
+                    out=acc[:, j, :],
+                    lhsT=pw_codes[:, j * P : (j + 1) * P].bitcast(FP8X4),
+                    lhsT_scale=pw_scales[:, j * P : (j + 1) * P],
+                    rhs=a_codes[c][:, q * P : (q + 1) * P].bitcast(FP8X4),
+                    rhs_scale=a_scales[c][:, q * P : (q + 1) * P],
+                    start=True,
+                    stop=True,
+                )
+            dyn[c, q] = acc
 
         def transpose_x(c, u):
             if not live(c):
@@ -238,68 +233,55 @@ def tile_dssattention_pa_t_kernel(tc, wv, x, dw_w, dw_b, pw_w, pw_b, p_w1, out):
                 )
             x_t[c, u] = bank
 
-        def copy_x(c, u):
+        def bias_x(c, u):
             if not live(c):
                 return
             if u == 0:
-                words = work.tile([P, 2, CHUNK], F32, tag="x_words")
-                x_words[c] = words
-            nc.scalar.copy(out=x_words[c][:, u, :], in_=x_t[c, u][:])
+                biased = work.tile([P, PACK, CHUNK], F32, tag="x_biased")
+                x_biased[c] = biased
+            halves = x_t[c, u][:].bitcast(BF16).rearrange("p (w e) -> p w e", e=2)
+            for e in range(2):
+                nc.scalar.activation(
+                    out=x_biased[c][:, 2 * u + e, :],
+                    in_=halves[:, :, e],
+                    func=IDENTITY,
+                    bias=bias_y[:, u, e : e + 1],
+                )
 
-        def add_x(c, j):
+        def add(c, q):
             if not live(c):
                 return
-            if j == 0:
-                planes = work.tile([P, PACK, CHUNK], BF16, tag="y_planes")
-                y_planes[c] = planes
-            u, e = divmod(j, 2)
-            nc.vector.scalar_tensor_tensor(
-                out=y_planes[c][:, j, :],
-                in0=dyn[c, j][:],
-                scalar=bias_y[:, u, e : e + 1],
-                in1=x_words[c][:].bitcast(BF16).rearrange("p u (w e) -> p u w e", e=2)[:, u, :, e],
-                op0=ADD,
-                op1=ADD,
+            if q == 0:
+                grouped = work.tile([P, CHUNK, PACK], BF16, tag="y_grouped", align_bytes=64)
+                y_grouped[c] = grouped
+            tokens = slice(q * P, (q + 1) * P)
+            nc.vector.tensor_tensor(
+                out=y_grouped[c][:, tokens, :].rearrange("p (c i) t -> p c t i", i=RUN),
+                in0=dyn[c, q][:].rearrange("p t (c i) -> p c t i", i=RUN),
+                in1=x_biased[c][:, :, tokens].rearrange("p t (c i) -> p c t i", i=RUN),
+                op=ADD,
             )
 
-        def group_y(c):
-            if not live(c):
-                return
-            grouped = work.tile([P, CHUNK, PACK], BF16, tag="y_grouped", align_bytes=64)
-            y_grouped[c] = grouped
-            if c == N_CHUNKS - 1:
-                for h in range(2):
-                    tokens = slice(h * HALF, (h + 1) * HALF)
-                    nc.vector.tensor_copy(
-                        out=grouped[:, tokens, :].rearrange("p (c i) t -> p c t i", i=4),
-                        in_=y_planes[c][:, :, tokens].rearrange("p t (c i) -> p c t i", i=4),
-                    )
-                return
-            nc.gpsimd.tensor_scalar(
-                out=grouped[:],
-                in0=y_planes[c][:].rearrange("p t w -> p w t"),
-                scalar1=1.0,
-                scalar2=0.0,
-                op0=MULT,
-                op1=ADD,
-            )
-
-        def quantise_y(c):
-            if not live(c):
-                return
+        def y_tiles(c):
             codes = work.tile([P, CHUNK], U32, tag="y_codes", align_bytes=64)
             scales = work.tile([P, CHUNK], U8, tag="y_scales", align_bytes=64)
             y_codes[c], y_scales[c] = codes, scales
-            if c == N_CHUNKS - 1:
-                for h in range(2):
-                    tokens = slice(h * HALF, (h + 1) * HALF)
-                    nc.vector.quantize_mx(
-                        out=codes[:, tokens].bitcast(FP8X4),
-                        scales=scales[:, tokens],
-                        in_=y_grouped[c][:, tokens, :].rearrange("p w t -> p (w t)"),
-                    )
+
+        def quantise_y(c):
+            if not live(c) or c == LAST:
                 return
-            quantise(codes, scales, y_grouped[c])
+            y_tiles(c)
+            quantise(y_codes[c], y_scales[c], y_grouped[c])
+
+        def quantise_y_half(c, h):
+            if h == 0:
+                y_tiles(c)
+            tokens = slice(h * HALF, (h + 1) * HALF)
+            nc.vector.quantize_mx(
+                out=y_codes[c][:, tokens].bitcast(FP8X4),
+                scales=y_scales[c][:, tokens],
+                in_=y_grouped[c][:, tokens, :].rearrange("p w t -> p (w t)"),
+            )
 
         def second_matmul(c):
             if not live(c):
@@ -334,38 +316,42 @@ def tile_dssattention_pa_t_kernel(tc, wv, x, dw_w, dw_b, pw_w, pw_b, p_w1, out):
 
         def step(n):
             load_wv(n + 3)
-            load_x(n)
+            load_x(n + 1)
 
-            group_y(n - 4)
-            copy_x(n - 3, 1)
+            bias_x(n - 2, 1)
+            if n - 3 == LAST:
+                quantise_y(n - 4)
             first_matmul(n - 3, 0)
             first_matmul(n - 3, 1)
+            add(n - 3, 0)
             affine(n, 0)
             transpose_wv(n, 1)
-            transpose_x(n - 2, 0)
-            group_a(n - 1, 0)
-            add_x(n - 3, 0)
-            add_x(n - 3, 1)
+            affine(n, 1)
+            transpose_x(n - 1, 0)
+            bias_x(n - 1, 0)
+            add(n - 3, 1)
 
             first_matmul(n - 3, 2)
             first_matmul(n - 3, 3)
             second_matmul(n - 5)
-            affine(n, 1)
             transpose_wv(n + 1, 0)
-            transpose_x(n - 2, 1)
-            group_a(n - 1, 1)
-            copy_x(n - 2, 0)
-            add_x(n - 3, 2)
-            add_x(n - 3, 3)
-            quantise_a(n - 2)
-            quantise_y(n - 4)
+            transpose_x(n - 1, 1)
+            add(n - 3, 2)
+            if n - 3 == LAST:
+                quantise_y_half(LAST, 0)
+            add(n - 3, 3)
+            if n - 3 == LAST:
+                quantise_y_half(LAST, 1)
+            else:
+                quantise_y(n - 4)
+            quantise_a(n - 1)
+            group_a(n)
             store(n - 5)
 
         step(-1)
         step(0)
         lay_out_weights()
         step(1)
-        step(2)
         quantise_weights()
-        for n in range(3, N_CHUNKS + 5):
+        for n in range(2, N_CHUNKS + 5):
             step(n)

@@ -23,6 +23,7 @@ HALF = CHUNK // 2
 N_CHUNKS = TOKENS // CHUNK
 RUN = 4
 LAST = N_CHUNKS - 1
+VECTOR_AFFINE = 2
 
 FLOPS = 2 * TOKENS * CHANNELS * CHANNELS + 2 * TOKENS * CHANNELS * RANK
 
@@ -81,15 +82,15 @@ def tile_dssattention_pa_t_kernel(tc, wv, x, dw_w, dw_b, pw_w, pw_b, p_w1, out):
             x_rows[c] = rows
 
 
+        vectors = const.tile([P, CHANNELS], BF16)
+        nc.gpsimd.memset(vectors[:], 0.0)
+        for row, vector in enumerate((dw_w, dw_b, pw_b)):
+            nc.sync.dma_start(out=vectors[row : row + 1, :], in_=vector.rearrange("(o k) -> o k", o=1))
+
         ident_bf16 = const.tile([P, P], BF16)
         masks.make_identity(nc, ident_bf16[:])
         ident_f32 = const.tile([P, P], F32)
         masks.make_identity(nc, ident_f32[:])
-
-        vectors = const.tile([P, CHANNELS], BF16)
-        nc.vector.memset(vectors[:], 0.0)
-        for row, vector in enumerate((dw_w, dw_b, pw_b)):
-            nc.sync.dma_start(out=vectors[row : row + 1, :], in_=vector.rearrange("(o k) -> o k", o=1))
 
         load_wv(0)
         pw_rows = const.tile([P, PACK, CHANNELS], BF16)
@@ -98,9 +99,13 @@ def tile_dssattention_pa_t_kernel(tc, wv, x, dw_w, dw_b, pw_w, pw_b, p_w1, out):
                 out=pw_rows[:, 2 * u : 2 * u + 2, :],
                 in_=pw_w[256 * u : 256 * (u + 1), :].rearrange("(m e) k -> m e k", e=2),
             )
+        load_x(0)
         load_wv(1)
         p1_rows = const.tile([P, CHANNELS], BF16)
         nc.sync.dma_start(out=p1_rows[:], in_=p_w1)
+        load_x(1)
+        load_wv(2)
+        load_x(2)
 
         vectors_t = psum_dyn.tile([P, 2, CHUNK], BF16, tag="dyn")
         for t in range(PACK):
@@ -127,16 +132,28 @@ def tile_dssattention_pa_t_kernel(tc, wv, x, dw_w, dw_b, pw_w, pw_b, p_w1, out):
         pw_codes = const.tile([P, CHUNK], U32, align_bytes=64)
         pw_scales = const.tile([P, CHUNK], U8, align_bytes=64)
 
-        pw_planes = const.tile([P, PACK, CHUNK], BF16)
         pw_grouped = const.tile([P, CHUNK, PACK], BF16, align_bytes=64)
         p1_grouped = const.tile([P, RANK, PACK], BF16, align_bytes=64)
 
-        def lay_out_weights():
-            for h in range(2):
-                bank = psum_dyn.tile([P, 2, CHUNK], BF16, tag="dyn")
-                transpose_channel_planes(bank, pw_rows, h)
-                nc.scalar.copy(out=pw_planes[:, 2 * h : 2 * h + 2, :], in_=bank[:])
-            nc.vector.tensor_copy(out=pw_grouped[:], in_=pw_planes[:].rearrange("p t w -> p w t"))
+        def lay_out_pw(h, copy):
+            bank = psum_dyn.tile([P, PACK, HALF], BF16, tag="dyn")
+            for t in range(PACK):
+                for i in range(2):
+                    nc.tensor.transpose(
+                        bank[:, t, i * P : (i + 1) * P], pw_rows[:, 2 * h + i, t * P : (t + 1) * P], ident_bf16[:]
+                    )
+            rows = slice(h * HALF, (h + 1) * HALF)
+            copy(out=pw_grouped[:, rows, :], in_=bank[:].rearrange("p t w -> p w t"))
+
+        def quantise_pw(h):
+            rows = slice(h * HALF, (h + 1) * HALF)
+            nc.vector.quantize_mx(
+                out=pw_codes[:, rows].bitcast(FP8X4),
+                scales=pw_scales[:, rows],
+                in_=pw_grouped[:, rows, :].rearrange("p w t -> p (w t)"),
+            )
+
+        def lay_out_p1():
             p1_t = psum_out.tile([P, 2, RANK], F32, tag="out_acc")
             for u in range(2):
                 nc.tensor.transpose(p1_t[:, u, :], p1_rows[:].bitcast(F32)[:, u * P : (u + 1) * P], ident_f32[:])
@@ -144,10 +161,6 @@ def tile_dssattention_pa_t_kernel(tc, wv, x, dw_w, dw_b, pw_w, pw_b, p_w1, out):
                 out=p1_grouped[:].rearrange("p r t -> p (r t)").bitcast(F32).rearrange("p (r u) -> p r u", u=2),
                 in_=p1_t[:].rearrange("p u r -> p r u"),
             )
-
-        def quantise_weights():
-            quantise(pw_codes, pw_scales, pw_grouped)
-            quantise(p1_codes, p1_scales, p1_grouped)
 
 
         def transpose_wv(c, h):
@@ -160,12 +173,12 @@ def tile_dssattention_pa_t_kernel(tc, wv, x, dw_w, dw_b, pw_w, pw_b, p_w1, out):
         def affine(c, h):
             if not live(c):
                 return
-            if h == 0:
+            if c not in a_planes:
                 planes = work.tile([P, PACK, CHUNK], BF16, tag="a_planes")
                 a_planes[c] = planes
             for i in range(2):
                 t = 2 * h + i
-                if h == 0:
+                if h == 0 or c < VECTOR_AFFINE:
                     nc.vector.tensor_scalar(
                         out=a_planes[c][:, t, :],
                         in0=wv_t[c, h][:, i, :],
@@ -187,6 +200,16 @@ def tile_dssattention_pa_t_kernel(tc, wv, x, dw_w, dw_b, pw_w, pw_b, p_w1, out):
             if not live(c):
                 return
             grouped = work.tile([P, CHUNK, PACK], BF16, tag="a_grouped", bufs=1, align_bytes=64)
+            a_grouped[c] = grouped
+            if c == 0:
+                nc.vector.tensor_copy(out=grouped[:], in_=a_planes[c][:].rearrange("p t w -> p w t"))
+                return
+            if c == LAST:
+                nc.scalar.copy(
+                    out=grouped[:].rearrange("p (c i) t -> p c t i", i=RUN),
+                    in_=a_planes[c][:].rearrange("p t (c i) -> p c t i", i=RUN),
+                )
+                return
             nc.gpsimd.tensor_scalar(
                 out=grouped[:],
                 in0=a_planes[c][:].rearrange("p t w -> p w t"),
@@ -195,7 +218,6 @@ def tile_dssattention_pa_t_kernel(tc, wv, x, dw_w, dw_b, pw_w, pw_b, p_w1, out):
                 op0=MULT,
                 op1=ADD,
             )
-            a_grouped[c] = grouped
 
         def quantise_a(c):
             if not live(c):
@@ -273,10 +295,10 @@ def tile_dssattention_pa_t_kernel(tc, wv, x, dw_w, dw_b, pw_w, pw_b, p_w1, out):
             y_tiles(c)
             quantise(y_codes[c], y_scales[c], y_grouped[c])
 
-        def quantise_y_half(c, h):
-            if h == 0:
+        def quantise_y_tiles(c, first, count):
+            if first == 0:
                 y_tiles(c)
-            tokens = slice(h * HALF, (h + 1) * HALF)
+            tokens = slice(first * P, (first + count) * P)
             nc.vector.quantize_mx(
                 out=y_codes[c][:, tokens].bitcast(FP8X4),
                 scales=y_scales[c][:, tokens],
@@ -288,70 +310,120 @@ def tile_dssattention_pa_t_kernel(tc, wv, x, dw_w, dw_b, pw_w, pw_b, p_w1, out):
                 return
             acc = psum_out.tile([P, TILES, RANK], F32, tag="out_acc")
             for q in range(TILES):
-                nc.tensor.matmul_mx(
-                    out=acc[:, q, :],
-                    lhsT=y_codes[c][:, q * P : (q + 1) * P].bitcast(FP8X4),
-                    lhsT_scale=y_scales[c][:, q * P : (q + 1) * P],
-                    rhs=p1_codes[:].bitcast(FP8X4),
-                    rhs_scale=p1_scales[:],
-                    start=True,
-                    stop=True,
-                )
+                second_pass(acc[:, q, :], c, q)
             out_acc[c] = acc
+
+        def second_pass(acc, c, q):
+            nc.tensor.matmul_mx(
+                out=acc,
+                lhsT=y_codes[c][:, q * P : (q + 1) * P].bitcast(FP8X4),
+                lhsT_scale=y_scales[c][:, q * P : (q + 1) * P],
+                rhs=p1_codes[:].bitcast(FP8X4),
+                rhs_scale=p1_scales[:],
+                start=True,
+                stop=True,
+            )
 
         def store(c):
             if not live(c):
                 return
             result = work.tile([P, TILES, RANK], F32, tag="result")
-            pieces = 2 if c == N_CHUNKS - 1 else 1
-            width = TILES // pieces
-            for i in range(pieces):
-                tiles = slice(i * width, (i + 1) * width)
-                nc.scalar.copy(out=result[:, tiles, :], in_=out_acc[c][:, tiles, :])
-                nc.sync.dma_start(
-                    out=out_chunks[c][:, i * width * RANK : (i + 1) * width * RANK],
-                    in_=result[:, tiles, :].rearrange("p q r -> p (q r)"),
-                )
+            nc.scalar.copy(out=result[:], in_=out_acc[c][:])
+            nc.sync.dma_start(out=out_chunks[c], in_=result[:].rearrange("p q r -> p (q r)"))
 
+        def finish(c, first, count):
+            result = work.tile([P, count, RANK], F32, tag="result_part")
+            acc = psum_dyn.tile([P, count, RANK], F32, tag="dyn")
+            for i in range(count):
+                second_pass(acc[:, i, :], c, first + i)
+            nc.scalar.copy(out=result[:], in_=acc[:])
+            nc.sync.dma_start(
+                out=out_chunks[c][:, first * RANK : (first + count) * RANK], in_=result[:].rearrange("p q r -> p (q r)")
+            )
+
+
+        def transpose_chunk(c):
+            for h in range(2):
+                transpose_wv(c, h)
+            transpose_x(c, 0)
 
         def step(n):
-            load_wv(n + 3)
-            load_x(n + 1)
+            load_wv(n + 2)
+            load_x(n + 2)
 
-            bias_x(n - 2, 1)
-            if n - 3 == LAST:
-                quantise_y(n - 4)
-            first_matmul(n - 3, 0)
-            first_matmul(n - 3, 1)
-            add(n - 3, 0)
-            affine(n, 0)
-            transpose_wv(n, 1)
-            affine(n, 1)
-            transpose_x(n - 1, 0)
-            bias_x(n - 1, 0)
-            add(n - 3, 1)
-
-            first_matmul(n - 3, 2)
-            first_matmul(n - 3, 3)
-            second_matmul(n - 5)
-            transpose_wv(n + 1, 0)
-            transpose_x(n - 1, 1)
+            if n > 2:
+                first_matmul(n - 2, 0)
+                first_matmul(n - 2, 1)
+            transpose_x(n, 1)
             add(n - 3, 2)
-            if n - 3 == LAST:
-                quantise_y_half(LAST, 0)
             add(n - 3, 3)
-            if n - 3 == LAST:
-                quantise_y_half(LAST, 1)
-            else:
-                quantise_y(n - 4)
+            affine(n, 1)
+            bias_x(n, 0)
+            bias_x(n, 1)
+            first_matmul(n - 2, 2)
+            add(n - 2, 0)
+            first_matmul(n - 2, 3)
+            second_matmul(n - 4)
+            affine(n, 0)
+            transpose_chunk(n + 1)
+            add(n - 2, 1)
+            quantise_y(n - 3)
             quantise_a(n - 1)
             group_a(n)
-            store(n - 5)
+            store(n - 4)
 
-        step(-1)
-        step(0)
-        lay_out_weights()
-        step(1)
-        quantise_weights()
-        for n in range(2, N_CHUNKS + 5):
+        transpose_wv(0, 0)
+        affine(0, 0)
+        transpose_wv(0, 1)
+        affine(0, 1)
+        group_a(0)
+        lay_out_pw(0, nc.scalar.copy)
+        lay_out_pw(1, nc.vector.tensor_copy)
+        for u in range(2):
+            transpose_x(0, u)
+            bias_x(0, u)
+        transpose_wv(1, 0)
+        transpose_wv(1, 1)
+        lay_out_p1()
+        transpose_x(1, 0)
+        transpose_x(1, 1)
+        quantise_pw(0)
+        quantise_a(0)
+        quantise_pw(1)
+        load_wv(3)
+        load_x(3)
+        affine(1, 0)
+        affine(1, 1)
+        bias_x(1, 0)
+        bias_x(1, 1)
+        group_a(1)
+        first_matmul(0, 0)
+        first_matmul(0, 1)
+        transpose_chunk(2)
+
+        step(2)
+        quantise(p1_codes, p1_scales, p1_grouped)
+        for n in range(3, N_CHUNKS + 1):
             step(n)
+
+        first_matmul(LAST, 0)
+        add(LAST - 1, 2)
+        first_matmul(LAST, 1)
+        add(LAST - 1, 3)
+        second_matmul(LAST - 2)
+        store(LAST - 2)
+        add(LAST, 0)
+        quantise_y(LAST - 1)
+        first_matmul(LAST, 2)
+        first_matmul(LAST, 3)
+        add(LAST, 1)
+        second_matmul(LAST - 1)
+        store(LAST - 1)
+        add(LAST, 2)
+        quantise_y_tiles(LAST, 0, 2)
+        add(LAST, 3)
+        quantise_y_tiles(LAST, 2, 1)
+        quantise_y_tiles(LAST, 3, 1)
+        finish(LAST, 0, 2)
+        finish(LAST, 2, 1)
+        finish(LAST, 3, 1)

@@ -23,6 +23,7 @@ HALF = CHUNK // 2
 N_CHUNKS = TOKENS // CHUNK
 RUN = 4
 LAST = N_CHUNKS - 1
+VECTOR_TOKENS = 192
 VECTOR_AFFINE = 2
 
 FLOPS = 2 * TOKENS * CHANNELS * CHANNELS + 2 * TOKENS * CHANNELS * RANK
@@ -170,31 +171,44 @@ def tile_dssattention_pa_t_kernel(tc, wv, x, dw_w, dw_b, pw_w, pw_b, p_w1, out):
             transpose_channel_planes(bank, wv_rows[c], h)
             wv_t[c, h] = bank
 
+        def vector_affine(c, t, tokens):
+            nc.vector.tensor_scalar(
+                out=a_planes[c][:, t, tokens],
+                in0=wv_t[c, t // 2][:, t % 2, tokens],
+                scalar1=affine_consts[:, t, 0:1],
+                scalar2=affine_consts[:, t, 1:2],
+                op0=MULT,
+                op1=ADD,
+            )
+
+        def scalar_affine(c, t, tokens):
+            nc.scalar.activation(
+                out=a_planes[c][:, t, tokens],
+                in_=wv_t[c, t // 2][:, t % 2, tokens],
+                func=IDENTITY,
+                scale=affine_consts[:, t, 0:1],
+                bias=affine_consts[:, t, 1:2],
+            )
+
         def affine(c, h):
             if not live(c):
                 return
             if c not in a_planes:
                 planes = work.tile([P, PACK, CHUNK], BF16, tag="a_planes")
                 a_planes[c] = planes
-            for i in range(2):
-                t = 2 * h + i
-                if h == 0 or c < VECTOR_AFFINE:
-                    nc.vector.tensor_scalar(
-                        out=a_planes[c][:, t, :],
-                        in0=wv_t[c, h][:, i, :],
-                        scalar1=affine_consts[:, t, 0:1],
-                        scalar2=affine_consts[:, t, 1:2],
-                        op0=MULT,
-                        op1=ADD,
-                    )
-                else:
-                    nc.scalar.activation(
-                        out=a_planes[c][:, t, :],
-                        in_=wv_t[c, h][:, i, :],
-                        func=IDENTITY,
-                        scale=affine_consts[:, t, 0:1],
-                        bias=affine_consts[:, t, 1:2],
-                    )
+            everything = slice(0, CHUNK)
+            if h == 0:
+                vector_affine(c, 0, everything)
+                vector_affine(c, 1, everything)
+            if c < VECTOR_AFFINE:
+                if h == 1:
+                    vector_affine(c, 2, everything)
+                    vector_affine(c, 3, everything)
+            elif h == 1:
+                scalar_affine(c, 2, slice(VECTOR_TOKENS, CHUNK))
+                scalar_affine(c, 3, everything)
+            else:
+                vector_affine(c, 2, slice(0, VECTOR_TOKENS))
 
         def group_a(c):
             if not live(c):

@@ -356,11 +356,6 @@ def tile_dssattention_pa_t_kernel(tc, wv, x, dw_w, dw_b, pw_w, pw_b, p_w1, out):
             )
 
 
-        def transpose_chunk(c):
-            for h in range(2):
-                transpose_wv(c, h)
-            transpose_x(c, 0)
-
         def step(n):
             load_wv(n + 2)
             load_x(n + 2)
@@ -368,18 +363,20 @@ def tile_dssattention_pa_t_kernel(tc, wv, x, dw_w, dw_b, pw_w, pw_b, p_w1, out):
             if n > 2:
                 first_matmul(n - 2, 0)
                 first_matmul(n - 2, 1)
-            transpose_x(n, 1)
             add(n - 3, 2)
             add(n - 3, 3)
             affine(n, 1)
             bias_x(n, 0)
+            transpose_x(n, 1)
+            transpose_wv(n + 1, 1)
             bias_x(n, 1)
+            affine(n, 0)
             first_matmul(n - 2, 2)
             add(n - 2, 0)
             first_matmul(n - 2, 3)
             second_matmul(n - 4)
-            affine(n, 0)
-            transpose_chunk(n + 1)
+            transpose_wv(n + 1, 0)
+            transpose_x(n + 1, 0)
             add(n - 2, 1)
             quantise_y(n - 3)
             quantise_a(n - 1)
@@ -413,7 +410,9 @@ def tile_dssattention_pa_t_kernel(tc, wv, x, dw_w, dw_b, pw_w, pw_b, p_w1, out):
         group_a(1)
         first_matmul(0, 0)
         first_matmul(0, 1)
-        transpose_chunk(2)
+        transpose_wv(2, 1)
+        transpose_wv(2, 0)
+        transpose_x(2, 0)
 
         step(2)
         quantise(p1_codes, p1_scales, p1_grouped)

@@ -24,7 +24,7 @@ N_CHUNKS = TOKENS // CHUNK
 RUN = 4
 LAST = N_CHUNKS - 1
 VECTOR_TOKENS = 192
-VECTOR_AFFINE = 2
+VECTOR_AFFINE = 3
 
 FLOPS = 2 * TOKENS * CHANNELS * CHANNELS + 2 * TOKENS * CHANNELS * RANK
 
@@ -213,20 +213,18 @@ def tile_dssattention_pa_t_kernel(tc, wv, x, dw_w, dw_b, pw_w, pw_b, p_w1, out):
         def group_a(c):
             if not live(c):
                 return
-            grouped = work.tile([P, CHUNK, PACK], BF16, tag="a_grouped", bufs=1, align_bytes=64)
+            grouped = work.tile([P, CHUNK, PACK], BF16, tag="grouped", bufs=3, align_bytes=64)
             a_grouped[c] = grouped
-            if c == 0:
-                nc.vector.tensor_copy(out=grouped[:], in_=a_planes[c][:].rearrange("p t w -> p w t"))
-                return
+            tokens = slice(0, CHUNK)
             if c == LAST:
+                tokens = slice(0, HALF)
                 nc.scalar.copy(
-                    out=grouped[:].rearrange("p (c i) t -> p c t i", i=RUN),
-                    in_=a_planes[c][:].rearrange("p t (c i) -> p c t i", i=RUN),
+                    out=grouped[:, HALF:, :].rearrange("p (c i) t -> p c t i", i=RUN),
+                    in_=a_planes[c][:, :, HALF:].rearrange("p t (c i) -> p c t i", i=RUN),
                 )
-                return
             nc.gpsimd.tensor_scalar(
-                out=grouped[:],
-                in0=a_planes[c][:].rearrange("p t w -> p w t"),
+                out=grouped[:, tokens, :],
+                in0=a_planes[c][:, :, tokens].rearrange("p t w -> p w t"),
                 scalar1=1.0,
                 scalar2=0.0,
                 op0=MULT,
@@ -288,7 +286,7 @@ def tile_dssattention_pa_t_kernel(tc, wv, x, dw_w, dw_b, pw_w, pw_b, p_w1, out):
             if not live(c):
                 return
             if q == 0:
-                grouped = work.tile([P, CHUNK, PACK], BF16, tag="y_grouped", align_bytes=64)
+                grouped = work.tile([P, CHUNK, PACK], BF16, tag="grouped", bufs=3, align_bytes=64)
                 y_grouped[c] = grouped
             tokens = slice(q * P, (q + 1) * P)
             nc.vector.tensor_tensor(
@@ -360,19 +358,23 @@ def tile_dssattention_pa_t_kernel(tc, wv, x, dw_w, dw_b, pw_w, pw_b, p_w1, out):
             load_wv(n + 2)
             load_x(n + 2)
 
-            if n > 2:
+            if n > 3:
                 first_matmul(n - 2, 0)
                 first_matmul(n - 2, 1)
-            add(n - 3, 2)
-            add(n - 3, 3)
+                add(n - 3, 2)
+                add(n - 3, 3)
+            else:
+                add(n - 2, 0)
             affine(n, 1)
             bias_x(n, 0)
             transpose_x(n, 1)
             transpose_wv(n + 1, 1)
             bias_x(n, 1)
-            affine(n, 0)
+            if n > 3:
+                affine(n, 0)
             first_matmul(n - 2, 2)
-            add(n - 2, 0)
+            if n > 3:
+                add(n - 2, 0)
             first_matmul(n - 2, 3)
             second_matmul(n - 4)
             transpose_wv(n + 1, 0)
@@ -398,24 +400,41 @@ def tile_dssattention_pa_t_kernel(tc, wv, x, dw_w, dw_b, pw_w, pw_b, p_w1, out):
         lay_out_p1()
         transpose_x(1, 0)
         transpose_x(1, 1)
-        quantise_pw(0)
-        quantise_a(0)
-        quantise_pw(1)
         load_wv(3)
         load_x(3)
         affine(1, 0)
         affine(1, 1)
+        quantise_pw(0)
+        quantise_a(0)
+        quantise_pw(1)
+        quantise(p1_codes, p1_scales, p1_grouped)
         bias_x(1, 0)
         bias_x(1, 1)
         group_a(1)
-        first_matmul(0, 0)
-        first_matmul(0, 1)
-        transpose_wv(2, 1)
+        for q in range(3):
+            first_matmul(0, q)
         transpose_wv(2, 0)
+        transpose_wv(2, 1)
         transpose_x(2, 0)
-
-        step(2)
-        quantise(p1_codes, p1_scales, p1_grouped)
+        load_wv(4)
+        load_x(4)
+        for q in range(3):
+            add(0, q)
+        first_matmul(0, 3)
+        quantise_a(1)
+        affine(2, 0)
+        affine(2, 1)
+        bias_x(2, 0)
+        transpose_x(2, 1)
+        bias_x(2, 1)
+        group_a(2)
+        add(0, 3)
+        transpose_wv(3, 0)
+        transpose_wv(3, 1)
+        affine(3, 0)
+        first_matmul(1, 0)
+        first_matmul(1, 1)
+        transpose_x(3, 0)
         for n in range(3, N_CHUNKS + 1):
             step(n)
 

@@ -23,8 +23,7 @@ HALF = CHUNK // 2
 N_CHUNKS = TOKENS // CHUNK
 RUN = 4
 LAST = N_CHUNKS - 1
-VECTOR_TOKENS = 192
-VECTOR_AFFINE = 3
+VECTOR_TOKENS = 128
 
 FLOPS = 2 * TOKENS * CHANNELS * CHANNELS + 2 * TOKENS * CHANNELS * RANK
 
@@ -83,6 +82,13 @@ def tile_dssattention_pa_t_kernel(tc, wv, x, dw_w, dw_b, pw_w, pw_b, p_w1, out):
             x_rows[c] = rows
 
 
+        first_rows = loads.tile([P, TILES, CHANNELS], BF16, tag="wv_rows")
+        for h in range(2):
+            columns = slice(h * 2 * P, (h + 1) * 2 * P)
+            nc.sync.dma_start(
+                out=first_rows[:, :, columns], in_=wv_chunks[0].rearrange("p (q k) -> p q k", q=TILES)[:, :, columns]
+            )
+        wv_rows[0] = first_rows
         vectors = const.tile([P, CHANNELS], BF16)
         nc.gpsimd.memset(vectors[:], 0.0)
         for row, vector in enumerate((dw_w, dw_b, pw_b)):
@@ -93,7 +99,6 @@ def tile_dssattention_pa_t_kernel(tc, wv, x, dw_w, dw_b, pw_w, pw_b, p_w1, out):
         ident_f32 = const.tile([P, P], F32)
         masks.make_identity(nc, ident_f32[:])
 
-        load_wv(0)
         pw_rows = const.tile([P, PACK, CHANNELS], BF16)
         for u in range(2):
             nc.sync.dma_start(
@@ -107,6 +112,10 @@ def tile_dssattention_pa_t_kernel(tc, wv, x, dw_w, dw_b, pw_w, pw_b, p_w1, out):
         load_x(1)
         load_wv(2)
         load_x(2)
+
+        bank = psum_wv.tile([P, 2, CHUNK], BF16, tag="wv_t")
+        transpose_channel_planes(bank, wv_rows[0], 0)
+        wv_t[0, 0] = bank
 
         vectors_t = psum_dyn.tile([P, 2, CHUNK], BF16, tag="dyn")
         for t in range(PACK):
@@ -171,44 +180,47 @@ def tile_dssattention_pa_t_kernel(tc, wv, x, dw_w, dw_b, pw_w, pw_b, p_w1, out):
             transpose_channel_planes(bank, wv_rows[c], h)
             wv_t[c, h] = bank
 
-        def vector_affine(c, t, tokens):
-            nc.vector.tensor_scalar(
-                out=a_planes[c][:, t, tokens],
-                in0=wv_t[c, t // 2][:, t % 2, tokens],
-                scalar1=affine_consts[:, t, 0:1],
-                scalar2=affine_consts[:, t, 1:2],
-                op0=MULT,
-                op1=ADD,
-            )
+        def vector_share(c, t):
+            if t < 2 or c < 2 or (t == 2 and c == 3):
+                return CHUNK
+            return VECTOR_TOKENS if t == 2 and 4 < c < N_CHUNKS - 3 else 0
 
-        def scalar_affine(c, t, tokens):
-            nc.scalar.activation(
-                out=a_planes[c][:, t, tokens],
-                in_=wv_t[c, t // 2][:, t % 2, tokens],
-                func=IDENTITY,
-                scale=affine_consts[:, t, 0:1],
-                bias=affine_consts[:, t, 1:2],
-            )
-
-        def affine(c, h):
-            if not live(c):
-                return
+        def planes_of(c):
             if c not in a_planes:
                 planes = work.tile([P, PACK, CHUNK], BF16, tag="a_planes")
                 a_planes[c] = planes
-            everything = slice(0, CHUNK)
-            if h == 0:
-                vector_affine(c, 0, everything)
-                vector_affine(c, 1, everything)
-            if c < VECTOR_AFFINE:
-                if h == 1:
-                    vector_affine(c, 2, everything)
-                    vector_affine(c, 3, everything)
-            elif h == 1:
-                scalar_affine(c, 2, slice(VECTOR_TOKENS, CHUNK))
-                scalar_affine(c, 3, everything)
-            else:
-                vector_affine(c, 2, slice(0, VECTOR_TOKENS))
+            return a_planes[c]
+
+        def vector_affine(c):
+            if not live(c):
+                return
+            planes = planes_of(c)
+            for t in range(PACK):
+                width = vector_share(c, t)
+                if width > 0:
+                    nc.vector.tensor_scalar(
+                        out=planes[:, t, :width],
+                        in0=wv_t[c, t // 2][:, t % 2, :width],
+                        scalar1=affine_consts[:, t, 0:1],
+                        scalar2=affine_consts[:, t, 1:2],
+                        op0=MULT,
+                        op1=ADD,
+                    )
+
+        def scalar_affine(c):
+            if not live(c):
+                return
+            planes = planes_of(c)
+            for t in range(PACK):
+                width = vector_share(c, t)
+                if width < CHUNK:
+                    nc.scalar.activation(
+                        out=planes[:, t, width:],
+                        in_=wv_t[c, t // 2][:, t % 2, width:],
+                        func=IDENTITY,
+                        scale=affine_consts[:, t, 0:1],
+                        bias=affine_consts[:, t, 1:2],
+                    )
 
         def group_a(c):
             if not live(c):
@@ -365,13 +377,14 @@ def tile_dssattention_pa_t_kernel(tc, wv, x, dw_w, dw_b, pw_w, pw_b, p_w1, out):
                 add(n - 3, 3)
             else:
                 add(n - 2, 0)
-            affine(n, 1)
+            if n > 3:
+                scalar_affine(n)
             bias_x(n, 0)
             transpose_x(n, 1)
             transpose_wv(n + 1, 1)
             bias_x(n, 1)
             if n > 3:
-                affine(n, 0)
+                vector_affine(n)
             first_matmul(n - 2, 2)
             if n > 3:
                 add(n - 2, 0)
@@ -380,15 +393,15 @@ def tile_dssattention_pa_t_kernel(tc, wv, x, dw_w, dw_b, pw_w, pw_b, p_w1, out):
             transpose_wv(n + 1, 0)
             transpose_x(n + 1, 0)
             add(n - 2, 1)
+            if n == 3:
+                quantise(p1_codes, p1_scales, p1_grouped)
             quantise_y(n - 3)
             quantise_a(n - 1)
             group_a(n)
             store(n - 4)
 
-        transpose_wv(0, 0)
-        affine(0, 0)
         transpose_wv(0, 1)
-        affine(0, 1)
+        vector_affine(0)
         group_a(0)
         lay_out_pw(0, nc.scalar.copy)
         lay_out_pw(1, nc.vector.tensor_copy)
@@ -402,12 +415,10 @@ def tile_dssattention_pa_t_kernel(tc, wv, x, dw_w, dw_b, pw_w, pw_b, p_w1, out):
         transpose_x(1, 1)
         load_wv(3)
         load_x(3)
-        affine(1, 0)
-        affine(1, 1)
+        vector_affine(1)
         quantise_pw(0)
         quantise_a(0)
         quantise_pw(1)
-        quantise(p1_codes, p1_scales, p1_grouped)
         bias_x(1, 0)
         bias_x(1, 1)
         group_a(1)
@@ -421,19 +432,20 @@ def tile_dssattention_pa_t_kernel(tc, wv, x, dw_w, dw_b, pw_w, pw_b, p_w1, out):
         for q in range(3):
             add(0, q)
         first_matmul(0, 3)
-        quantise_a(1)
-        affine(2, 0)
-        affine(2, 1)
+        vector_affine(2)
+        scalar_affine(2)
         bias_x(2, 0)
         transpose_x(2, 1)
         bias_x(2, 1)
+        quantise_a(1)
         group_a(2)
         add(0, 3)
         transpose_wv(3, 0)
         transpose_wv(3, 1)
-        affine(3, 0)
         first_matmul(1, 0)
         first_matmul(1, 1)
+        vector_affine(3)
+        scalar_affine(3)
         transpose_x(3, 0)
         for n in range(3, N_CHUNKS + 1):
             step(n)

from contextlib import ExitStack

import concourse.masks as masks
import concourse.mybir as mybir

F32 = mybir.dt.float32
BF16 = mybir.dt.bfloat16
U32 = mybir.dt.uint32
U8 = mybir.dt.uint8
FP8X4 = mybir.dt.float8_e4m3fn_x4
IDENTITY = mybir.ActivationFunctionType.Identity
ADD = mybir.AluOpType.add
MULT = mybir.AluOpType.mult

P = 128
PACK = 4
CHANNELS = P * PACK
RANK = 128
TOKENS = 32 * 256
CHUNK = 512
TILES = CHUNK // P
HALF = CHUNK // 2
N_CHUNKS = TOKENS // CHUNK
RUN = 4
LAST = N_CHUNKS - 1
VECTOR_TOKENS = 128

FLOPS = 2 * TOKENS * CHANNELS * CHANNELS + 2 * TOKENS * CHANNELS * RANK


def tile_dssattention_pa_t_kernel(tc, wv, x, dw_w, dw_b, pw_w, pw_b, p_w1, out):
    nc = tc.nc

    wv_chunks = wv.flatten_outer_dims().rearrange("(c p q) k -> c p (q k)", p=P, q=TILES)
    x_chunks = x.flatten_outer_dims().rearrange("(c p q) k -> c p (q k)", p=P, q=TILES)
    out_chunks = out.flatten_outer_dims().rearrange("(c p q) r -> c p (q r)", p=P, q=TILES)

    with ExitStack() as stack:
        const = stack.enter_context(tc.tile_pool(name="const", bufs=1))
        loads = stack.enter_context(tc.tile_pool(name="loads", bufs=4))
        work = stack.enter_context(tc.tile_pool(name="work", bufs=4))
        psum_wv = stack.enter_context(tc.psum_pool(name="psum_wv", bufs=2))
        psum_x = stack.enter_context(tc.psum_pool(name="psum_x", bufs=2))
        psum_dyn = stack.enter_context(tc.psum_pool(name="psum_dyn", bufs=3))
        psum_out = stack.enter_context(tc.psum_pool(name="psum_out", bufs=1))
        stack.enter_context(tc.manual_schedule())

        wv_rows, x_rows, wv_t, x_t, x_biased = {}, {}, {}, {}, {}
        a_planes, a_grouped, a_codes, a_scales = {}, {}, {}, {}
        dyn, y_grouped, y_codes, y_scales, out_acc = {}, {}, {}, {}, {}

        def live(c):
            return 0 <= c < N_CHUNKS

        def transpose_channel_planes(bank, rows, h):
            for i in range(2):
                t = 2 * h + i
                for q in range(TILES):
                    nc.tensor.transpose(
                        bank[:, i, q * P : (q + 1) * P], rows[:, q, t * P : (t + 1) * P], ident_bf16[:]
                    )

        def quantise(codes, scales, grouped):
            nc.vector.quantize_mx(
                out=codes[:].bitcast(FP8X4),
                scales=scales[:],
                in_=grouped[:].rearrange("p w t -> p (w t)"),
            )

        def load_wv(c):
            if not live(c):
                return
            rows = loads.tile([P, TILES, CHANNELS], BF16, tag="wv_rows")
            nc.sync.dma_start(out=rows[:].rearrange("p q k -> p (q k)"), in_=wv_chunks[c])
            wv_rows[c] = rows

        def load_x(c):
            if not live(c):
                return
            rows = loads.tile([P, TILES, CHANNELS], BF16, tag="x_rows")
            nc.sync.dma_start(out=rows[:].rearrange("p q k -> p (q k)"), in_=x_chunks[c])
            x_rows[c] = rows


        first_rows = loads.tile([P, TILES, CHANNELS], BF16, tag="wv_rows")
        for h in range(2):
            columns = slice(h * 2 * P, (h + 1) * 2 * P)
            nc.sync.dma_start(
                out=first_rows[:, :, columns], in_=wv_chunks[0].rearrange("p (q k) -> p q k", q=TILES)[:, :, columns]
            )
        wv_rows[0] = first_rows
        vectors = const.tile([P, CHANNELS], BF16)
        nc.gpsimd.memset(vectors[:], 0.0)
        for row, vector in enumerate((dw_w, dw_b, pw_b)):
            nc.sync.dma_start(out=vectors[row : row + 1, :], in_=vector.rearrange("(o k) -> o k", o=1))

        ident_bf16 = const.tile([P, P], BF16)
        masks.make_identity(nc, ident_bf16[:])
        ident_f32 = const.tile([P, P], F32)
        masks.make_identity(nc, ident_f32[:])

        pw_rows = const.tile([P, PACK, CHANNELS], BF16)
        for u in range(2):
            nc.sync.dma_start(
                out=pw_rows[:, 2 * u : 2 * u + 2, :],
                in_=pw_w[256 * u : 256 * (u + 1), :].rearrange("(m e) k -> m e k", e=2),
            )
        load_x(0)
        load_wv(1)
        p1_rows = const.tile([P, CHANNELS], BF16)
        nc.sync.dma_start(out=p1_rows[:], in_=p_w1)
        load_x(1)
        load_wv(2)
        load_x(2)

        bank = psum_wv.tile([P, 2, CHUNK], BF16, tag="wv_t")
        transpose_channel_planes(bank, wv_rows[0], 0)
        wv_t[0, 0] = bank

        vectors_t = psum_dyn.tile([P, 2, CHUNK], BF16, tag="dyn")
        for t in range(PACK):
            nc.tensor.transpose(
                vectors_t[:, 0, t * P : (t + 1) * P], vectors[:, t * P : (t + 1) * P], ident_bf16[:]
            )
        affine_consts = const.tile([P, PACK, 2], F32)
        nc.vector.tensor_copy(
            out=affine_consts[:], in_=vectors_t[:, 0, :].rearrange("p (t r) -> p t r", t=PACK)[:, :, 0:2]
        )
        vector_words_t = psum_dyn.tile([P, 2, P], F32, tag="dyn")
        for u in range(2):
            nc.tensor.transpose(
                vector_words_t[:, u, :], vectors[:].bitcast(F32)[:, u * P : (u + 1) * P], ident_f32[:]
            )
        bias_y = const.tile([P, 2, 2], F32)
        nc.vector.tensor_copy(
            out=bias_y[:],
            in_=vector_words_t[:].bitcast(BF16).rearrange("p u (r e) -> p u r e", e=2)[:, :, 2, :],
        )

        p1_codes = const.tile([P, RANK], U32, align_bytes=64)
        p1_scales = const.tile([P, RANK], U8, align_bytes=64)
        pw_codes = const.tile([P, CHUNK], U32, align_bytes=64)
        pw_scales = const.tile([P, CHUNK], U8, align_bytes=64)

        pw_grouped = const.tile([P, CHUNK, PACK], BF16, align_bytes=64)
        p1_grouped = const.tile([P, RANK, PACK], BF16, align_bytes=64)

        def lay_out_pw(h, copy):
            bank = psum_dyn.tile([P, PACK, HALF], BF16, tag="dyn")
            for t in range(PACK):
                for i in range(2):
                    nc.tensor.transpose(
                        bank[:, t, i * P : (i + 1) * P], pw_rows[:, 2 * h + i, t * P : (t + 1) * P], ident_bf16[:]
                    )
            rows = slice(h * HALF, (h + 1) * HALF)
            copy(out=pw_grouped[:, rows, :], in_=bank[:].rearrange("p t w -> p w t"))

        def quantise_pw(h):
            rows = slice(h * HALF, (h + 1) * HALF)
            nc.vector.quantize_mx(
                out=pw_codes[:, rows].bitcast(FP8X4),
                scales=pw_scales[:, rows],
                in_=pw_grouped[:, rows, :].rearrange("p w t -> p (w t)"),
            )

        def lay_out_p1():
            p1_t = psum_out.tile([P, 2, RANK], F32, tag="out_acc")
            for u in range(2):
                nc.tensor.transpose(p1_t[:, u, :], p1_rows[:].bitcast(F32)[:, u * P : (u + 1) * P], ident_f32[:])
            nc.scalar.copy(
                out=p1_grouped[:].rearrange("p r t -> p (r t)").bitcast(F32).rearrange("p (r u) -> p r u", u=2),
                in_=p1_t[:].rearrange("p u r -> p r u"),
            )


        def transpose_wv(c, h):
            if not live(c):
                return
            bank = psum_wv.tile([P, 2, CHUNK], BF16, tag="wv_t")
            transpose_channel_planes(bank, wv_rows[c], h)
            wv_t[c, h] = bank

        def vector_share(c, t):
            if t < 2 or c < 2 or (t == 2 and c == 3):
                return CHUNK
            return VECTOR_TOKENS if t == 2 and 4 < c < N_CHUNKS - 3 else 0

        def planes_of(c):
            if c not in a_planes:
                planes = work.tile([P, PACK, CHUNK], BF16, tag="a_planes")
                a_planes[c] = planes
            return a_planes[c]

        def vector_affine(c):
            if not live(c):
                return
            planes = planes_of(c)
            for t in range(PACK):
                width = vector_share(c, t)
                if width > 0:
                    nc.vector.tensor_scalar(
                        out=planes[:, t, :width],
                        in0=wv_t[c, t // 2][:, t % 2, :width],
                        scalar1=affine_consts[:, t, 0:1],
                        scalar2=affine_consts[:, t, 1:2],
                        op0=MULT,
                        op1=ADD,
                    )

        def scalar_affine(c):
            if not live(c):
                return
            planes = planes_of(c)
            for t in range(PACK):
                width = vector_share(c, t)
                if width < CHUNK:
                    nc.scalar.activation(
                        out=planes[:, t, width:],
                        in_=wv_t[c, t // 2][:, t % 2, width:],
                        func=IDENTITY,
                        scale=affine_consts[:, t, 0:1],
                        bias=affine_consts[:, t, 1:2],
                    )

        def group_a(c):
            if not live(c):
                return
            grouped = work.tile([P, CHUNK, PACK], BF16, tag="grouped", bufs=3, align_bytes=64)
            a_grouped[c] = grouped
            tokens = slice(0, CHUNK)
            if c == LAST:
                tokens = slice(0, HALF)
                nc.scalar.copy(
                    out=grouped[:, HALF:, :].rearrange("p (c i) t -> p c t i", i=RUN),
                    in_=a_planes[c][:, :, HALF:].rearrange("p t (c i) -> p c t i", i=RUN),
                )
            nc.gpsimd.tensor_scalar(
                out=grouped[:, tokens, :],
                in0=a_planes[c][:, :, tokens].rearrange("p t w -> p w t"),
                scalar1=1.0,
                scalar2=0.0,
                op0=MULT,
                op1=ADD,
            )

        def quantise_a(c):
            if not live(c):
                return
            codes = work.tile([P, CHUNK], U32, tag="a_codes", align_bytes=64)
            scales = work.tile([P, CHUNK], U8, tag="a_scales", align_bytes=64)
            quantise(codes, scales, a_grouped[c])
            a_codes[c], a_scales[c] = codes, scales

        def first_matmul(c, q):
            if not live(c):
                return
            acc = psum_dyn.tile([P, PACK, P], F32, tag="dyn")
            for j in range(PACK):
                nc.tensor.matmul_mx(
                    out=acc[:, j, :],
                    lhsT=pw_codes[:, j * P : (j + 1) * P].bitcast(FP8X4),
                    lhsT_scale=pw_scales[:, j * P : (j + 1) * P],
                    rhs=a_codes[c][:, q * P : (q + 1) * P].bitcast(FP8X4),
                    rhs_scale=a_scales[c][:, q * P : (q + 1) * P],
                    start=True,
                    stop=True,
                )
            dyn[c, q] = acc

        def transpose_x(c, u):
            if not live(c):
                return
            bank = psum_x.tile([P, CHUNK], F32, tag="x_t")
            for q in range(TILES):
                nc.tensor.transpose(
                    bank[:, q * P : (q + 1) * P],
                    x_rows[c][:].bitcast(F32)[:, q, u * P : (u + 1) * P],
                    ident_f32[:],
                )
            x_t[c, u] = bank

        def bias_x(c, u):
            if not live(c):
                return
            if u == 0:
                biased = work.tile([P, PACK, CHUNK], F32, tag="x_biased")
                x_biased[c] = biased
            halves = x_t[c, u][:].bitcast(BF16).rearrange("p (w e) -> p w e", e=2)
            for e in range(2):
                nc.scalar.activation(
                    out=x_biased[c][:, 2 * u + e, :],
                    in_=halves[:, :, e],
                    func=IDENTITY,
                    bias=bias_y[:, u, e : e + 1],
                )

        def add(c, q):
            if not live(c):
                return
            if q == 0:
                grouped = work.tile([P, CHUNK, PACK], BF16, tag="grouped", bufs=3, align_bytes=64)
                y_grouped[c] = grouped
            tokens = slice(q * P, (q + 1) * P)
            nc.vector.tensor_tensor(
                out=y_grouped[c][:, tokens, :].rearrange("p (c i) t -> p c t i", i=RUN),
                in0=dyn[c, q][:].rearrange("p t (c i) -> p c t i", i=RUN),
                in1=x_biased[c][:, :, tokens].rearrange("p t (c i) -> p c t i", i=RUN),
                op=ADD,
            )

        def y_tiles(c):
            codes = work.tile([P, CHUNK], U32, tag="y_codes", align_bytes=64)
            scales = work.tile([P, CHUNK], U8, tag="y_scales", align_bytes=64)
            y_codes[c], y_scales[c] = codes, scales

        def quantise_y(c):
            if not live(c) or c == LAST:
                return
            y_tiles(c)
            quantise(y_codes[c], y_scales[c], y_grouped[c])

        def quantise_y_tiles(c, first, count):
            if first == 0:
                y_tiles(c)
            tokens = slice(first * P, (first + count) * P)
            nc.vector.quantize_mx(
                out=y_codes[c][:, tokens].bitcast(FP8X4),
                scales=y_scales[c][:, tokens],
                in_=y_grouped[c][:, tokens, :].rearrange("p w t -> p (w t)"),
            )

        def second_matmul(c):
            if not live(c):
                return
            acc = psum_out.tile([P, TILES, RANK], F32, tag="out_acc")
            for q in range(TILES):
                second_pass(acc[:, q, :], c, q)
            out_acc[c] = acc

        def second_pass(acc, c, q):
            nc.tensor.matmul_mx(
                out=acc,
                lhsT=y_codes[c][:, q * P : (q + 1) * P].bitcast(FP8X4),
                lhsT_scale=y_scales[c][:, q * P : (q + 1) * P],
                rhs=p1_codes[:].bitcast(FP8X4),
                rhs_scale=p1_scales[:],
                start=True,
                stop=True,
            )

        def store(c):
            if not live(c):
                return
            result = work.tile([P, TILES, RANK], F32, tag="result")
            nc.scalar.copy(out=result[:], in_=out_acc[c][:])
            nc.sync.dma_start(out=out_chunks[c], in_=result[:].rearrange("p q r -> p (q r)"))

        def finish(c, first, count):
            result = work.tile([P, count, RANK], F32, tag="result_part")
            acc = psum_dyn.tile([P, count, RANK], F32, tag="dyn")
            for i in range(count):
                second_pass(acc[:, i, :], c, first + i)
            nc.scalar.copy(out=result[:], in_=acc[:])
            nc.sync.dma_start(
                out=out_chunks[c][:, first * RANK : (first + count) * RANK], in_=result[:].rearrange("p q r -> p (q r)")
            )


        def step(n):
            load_wv(n + 2)
            load_x(n + 2)

            if n > 3:
                first_matmul(n - 2, 0)
                first_matmul(n - 2, 1)
                add(n - 3, 2)
                add(n - 3, 3)
            else:
                add(n - 2, 0)
            if n > 3:
                scalar_affine(n)
            bias_x(n, 0)
            transpose_x(n, 1)
            transpose_wv(n + 1, 1)
            bias_x(n, 1)
            if n > 3:
                vector_affine(n)
            first_matmul(n - 2, 2)
            if n > 3:
                add(n - 2, 0)
            first_matmul(n - 2, 3)
            second_matmul(n - 4)
            transpose_wv(n + 1, 0)
            transpose_x(n + 1, 0)
            add(n - 2, 1)
            if n == 3:
                quantise(p1_codes, p1_scales, p1_grouped)
            quantise_y(n - 3)
            quantise_a(n - 1)
            group_a(n)
            store(n - 4)

        transpose_wv(0, 1)
        vector_affine(0)
        group_a(0)
        lay_out_pw(0, nc.scalar.copy)
        lay_out_pw(1, nc.vector.tensor_copy)
        for u in range(2):
            transpose_x(0, u)
            bias_x(0, u)
        transpose_wv(1, 0)
        transpose_wv(1, 1)
        lay_out_p1()
        transpose_x(1, 0)
        transpose_x(1, 1)
        load_wv(3)
        load_x(3)
        vector_affine(1)
        quantise_pw(0)
        quantise_a(0)
        quantise_pw(1)
        bias_x(1, 0)
        bias_x(1, 1)
        group_a(1)
        for q in range(3):
            first_matmul(0, q)
        transpose_wv(2, 0)
        transpose_wv(2, 1)
        transpose_x(2, 0)
        load_wv(4)
        load_x(4)
        for q in range(3):
            add(0, q)
        first_matmul(0, 3)
        vector_affine(2)
        scalar_affine(2)
        bias_x(2, 0)
        transpose_x(2, 1)
        bias_x(2, 1)
        quantise_a(1)
        group_a(2)
        add(0, 3)
        transpose_wv(3, 0)
        transpose_wv(3, 1)
        first_matmul(1, 0)
        first_matmul(1, 1)
        vector_affine(3)
        scalar_affine(3)
        transpose_x(3, 0)
        for n in range(3, N_CHUNKS + 1):
            step(n)

        first_matmul(LAST, 0)
        add(LAST - 1, 2)
        first_matmul(LAST, 1)
        add(LAST - 1, 3)
        second_matmul(LAST - 2)
        store(LAST - 2)
        add(LAST, 0)
        quantise_y(LAST - 1)
        first_matmul(LAST, 2)
        first_matmul(LAST, 3)
        add(LAST, 1)
        second_matmul(LAST - 1)
        store(LAST - 1)
        add(LAST, 2)
        quantise_y_tiles(LAST, 0, 2)
        add(LAST, 3)
        quantise_y_tiles(LAST, 2, 1)
        quantise_y_tiles(LAST, 3, 1)
        finish(LAST, 0, 2)
        finish(LAST, 2, 1)
        finish(LAST, 3, 1)
